import numpy as np
import ml_dtypes


def mxq(x, axis, fmt="e4m3"):
    dtype, down = {"e4m3": (ml_dtypes.float8_e4m3fn, 7), "e5m2": (ml_dtypes.float8_e5m2, 14)}[fmt]
    v = np.moveaxis(np.asarray(x, np.float32).astype(ml_dtypes.bfloat16).astype(np.float64), axis, -1)
    blocks = v.reshape(v.shape[:-1] + (-1, 32))
    amax = np.abs(blocks).max(-1, keepdims=True)
    byte = np.maximum(np.where(amax > 0, np.frexp(amax)[1] - 1 + 127, 0) - down, 1)
    scale = np.exp2(byte - 127.0)
    codes = (blocks / scale).astype(np.float32).astype(dtype).astype(np.float64)
    return np.moveaxis((codes * scale).reshape(v.shape), -1, axis)


WIDE = False


def mx_kscale(k):
    if not WIDE:
        return np.ones(k)
    levels = np.array([10, -10, 5, -5, 0])
    if k % 512:
        return np.exp2(np.random.permutation(np.resize(levels, k // 32))).repeat(32)
    a = np.empty((k // 512, 16))
    for p in range(k // 512):
        a[p, :8] = np.random.permutation(np.resize(levels, 8))
        for g in range(8):
            far = levels[np.abs(levels - a[p, g]) >= 10]
            a[p, g + 8] = far[np.random.randint(len(far))]
    return np.exp2(a.ravel()).repeat(32)


BF16 = ml_dtypes.bfloat16


def bf(x):
    return np.asarray(x, np.float32).astype(BF16)


def f64(x):
    return np.asarray(x).astype(np.float64)


B, N, J = 64, 512, 32
DECAY = 0.8


def decay_pattern(n, decay):
    i = np.arange(n)[:, None]
    j = np.arange(n)[None, :]
    w = np.where(j <= i, decay ** (1.0 * np.maximum(i - j, 0)), 0.0)
    return w / w.sum(axis=1, keepdims=True)


def setup_inputs():
    s = mx_kscale(N)
    x = np.random.standard_normal((B, N, J)) * (np.sqrt(N) / 8.0) * s.mean() / s[None, :, None]
    off = 1.5 * np.random.standard_normal((J, N, N)) + np.log(s)[None, None, :]
    pre = 8.0 * decay_pattern(N, DECAY) + 0.2 * np.random.standard_normal((N, N))
    return {"x": bf(x), "learnable_offset": bf(off), "predefined_weights": bf(pre)}


def reference(x, learnable_offset, predefined_weights):
    z = f64(predefined_weights)[None, :, :] + f64(learnable_offset)
    e = np.exp(z - z.max(-1, keepdims=True))
    masks = e / e.sum(-1, keepdims=True)
    y = mxq(f64(x), 1, "e4m3").transpose(2, 0, 1) @ mxq(masks, 2, "e4m3").transpose(0, 2, 1)
    return y.transpose(1, 2, 0)

@@ -1,0 +1,249 @@
+from contextlib import ExitStack
+
+import concourse.mybir as mybir
+from concourse.masks import make_identity
+
+FLOPS = 2 * 64 * 512 * 512 * 32
+
+BF16 = mybir.dt.bfloat16
+F32 = mybir.dt.float32
+U32 = mybir.dt.uint32
+U8 = mybir.dt.uint8
+FP8X4 = mybir.dt.float8_e4m3fn_x4
+ALU = mybir.AluOpType
+ACT = mybir.ActivationFunctionType
+AX = mybir.AxisListType
+
+P = 128
+B, N, J = 64, 512, 32
+NT = N // P
+PACK = 4
+JU = 4
+UNITS = [(a, j0) for a in range(NT) for j0 in range(0, J, JU)]
+NU = len(UNITS)
+UPA = J // JU
+
+PREFETCH = 6
+X_STEP = 7
+N_ON_V_FROM = 30
+C_SPLIT_FROM = 29
+
+
+def norm_on_vector(u, jj):
+    return u >= N_ON_V_FROM
+
+
+def step_tables():
+    s_n, s_c, s_q, s_mx = {}, {}, {}, {}
+    for u in range(NU):
+        s_n[u] = u + 1 if u >= N_ON_V_FROM else u + 2
+        s_c[u] = s_n[u] + 1
+        s_q[u] = s_c[u] + 1
+        early = X_STEP + 3 + u if u < UPA else X_STEP + 3 + UPA + (u - UPA) // 2
+        s_mx[u] = max(s_q[u] + 1, early)
+    return s_n, s_c, s_q, s_mx
+
+
+def tile_learnablemasktemporalaggregation_kernel(tc, x, learnable_offset, predefined_weights, out):
+    nc = tc.nc
+    off_v = learnable_offset.rearrange("j (a p) m -> a p j m", p=P)
+    pre_v = predefined_weights.rearrange("(a p) m -> p a m", p=P)
+    x_v = x.rearrange("b (p t) j -> p b t j", t=PACK)
+    out_v = out.rearrange("b (a p) j -> a p b j", p=P)
+    s_n, s_c, s_q, s_mx = step_tables()
+
+    with ExitStack() as ctx:
+        const = ctx.enter_context(tc.tile_pool(name="const", bufs=1))
+        ld = ctx.enter_context(tc.tile_pool(name="ld", bufs=PREFETCH + 1))
+        zp = ctx.enter_context(tc.tile_pool(name="zp", bufs=4))
+        st = ctx.enter_context(tc.tile_pool(name="st", bufs=6))
+        mp = ctx.enter_context(tc.tile_pool(name="mp", bufs=3))
+        gp = ctx.enter_context(tc.tile_pool(name="gp", bufs=3))
+        cp = ctx.enter_context(tc.tile_pool(name="cp", bufs=9))
+        op = ctx.enter_context(tc.tile_pool(name="op", bufs=2))
+        psum_c = ctx.enter_context(tc.psum_pool(name="psum_c", bufs=1))
+        psum_t = ctx.enter_context(tc.psum_pool(name="psum_t", bufs=4))
+        psum_o = ctx.enter_context(tc.psum_pool(name="psum_o", bufs=2))
+        ctx.enter_context(tc.manual_schedule())
+
+        off_t, z_t, nmax_t, ssum_t, rinv_t, mask_t = {}, {}, {}, {}, {}, {}
+        pt_t, grp_t, codes_t, scl_t, po_t, o_t = {}, {}, {}, {}, {}, {}
+
+        ident = const.tile([P, P], BF16)
+        make_identity(nc, ident[:])
+        pre_sb = const.tile([P, NT, N], BF16)
+        nc.sync.dma_start(out=pre_sb[:], in_=pre_v)
+        pre_ps = [psum_c.tile([P, 2, N], BF16, name="pre_ps%d" % i) for i in range(2)]
+        for a in range(NT):
+            nc.tensor.matmul(out=pre_ps[a // 2][:, a % 2, :], lhsT=ident[:], rhs=pre_sb[:, a, :], start=True, stop=True)
+
+        x_raw = const.tile([P, B * PACK, J], BF16)
+        x_grp = const.tile([P, J, B * PACK], BF16, align_bytes=64)
+        x_codes = const.tile([P, J * B], U32, align_bytes=64)
+        x_scl = const.tile([P, J * B], U8, align_bytes=64)
+
+        def x_load(c):
+            nc.sync.dma_start(
+                out=x_raw[:, 32 * c:32 * (c + 1), :].rearrange("p (b t) j -> p b t j", t=PACK),
+                in_=x_v[:, 8 * c:8 * (c + 1), :, :],
+            )
+
+        def x_group(c):
+            nc.gpsimd.tensor_scalar(
+                out=x_grp[:, JU * c:JU * (c + 1), :],
+                in0=x_raw[:, :, JU * c:JU * (c + 1)].rearrange("p c j -> p j c"),
+                scalar1=1.0, scalar2=0.0, op0=ALU.mult, op1=ALU.add,
+            )
+
+        def x_quant(c):
+            w = JU * B
+            nc.vector.quantize_mx(
+                out=x_codes[:, w * c:w * (c + 1)].bitcast(FP8X4),
+                scales=x_scl[:, w * c:w * (c + 1)],
+                in_=x_grp[:, JU * c:JU * (c + 1), :].rearrange("p j c -> p (j c)"),
+            )
+
+        def load(u):
+            a, j0 = UNITS[u]
+            off_t[u] = ld.tile([P, JU, N], BF16, name="off")
+            nc.sync.dma_start(out=off_t[u][:], in_=off_v[a][:, j0:j0 + JU, :])
+
+        def add_max(u):
+            a, j0 = UNITS[u]
+            z_t[u] = zp.tile([P, JU, N], F32, name="z")
+            nc.vector.tensor_tensor(
+                out=z_t[u][:], in0=off_t[u][:],
+                in1=pre_ps[a // 2][:, a % 2:a % 2 + 1, :].to_broadcast([P, JU, N]), op=ALU.add,
+            )
+            nmax_t[u] = st.tile([P, JU], F32, name="nmax")
+            nc.vector.tensor_reduce(out=nmax_t[u][:], in_=z_t[u][:], axis=AX.X, op=ALU.max, negate=True)
+
+        def exps(u):
+            ssum_t[u] = st.tile([P, JU], F32, name="ssum")
+            for jj in range(JU):
+                nc.scalar.activation(
+                    out=z_t[u][:, jj, :], in_=z_t[u][:, jj, :], func=ACT.Exp,
+                    bias=nmax_t[u][:, jj:jj + 1], scale=1.0, accum_out=ssum_t[u][:, jj:jj + 1],
+                )
+
+        def recip(u):
+            rinv_t[u] = st.tile([P, JU], F32, name="rinv")
+            nc.vector.reciprocal(out=rinv_t[u][:], in_=ssum_t[u][:])
+
+        def norm(u, on_vector):
+            if u not in mask_t:
+                mask_t[u] = mp.tile([P, JU, N], BF16, name="mask")
+            for jj in range(JU):
+                if norm_on_vector(u, jj) != on_vector:
+                    continue
+                if on_vector:
+                    nc.vector.tensor_scalar(
+                        out=mask_t[u][:, jj, :], in0=z_t[u][:, jj, :], scalar1=rinv_t[u][:, jj:jj + 1],
+                        scalar2=None, op0=ALU.mult,
+                    )
+                else:
+                    nc.gpsimd.tensor_scalar(
+                        out=mask_t[u][:, jj, :], in0=z_t[u][:, jj, :], scalar1=rinv_t[u][:, jj:jj + 1],
+                        scalar2=0.0, op0=ALU.mult, op1=ALU.add,
+                    )
+
+        def transp(u):
+            pt_t[u] = []
+            for half in range(2):
+                pt = psum_t.tile([P, 2, PACK, P], BF16, name="pt")
+                pt_t[u].append(pt)
+                for q in range(2):
+                    jj = 2 * half + q
+                    for t in range(PACK):
+                        nc.tensor.transpose(pt[:, q, t, :], mask_t[u][:, jj, t:N:PACK], ident[:])
+
+        def copy_out(u, half, on_vector):
+            if u not in grp_t:
+                grp_t[u] = gp.tile([P, JU, P, PACK], BF16, name="grp", align_bytes=64)
+            dst = grp_t[u][:, 2 * half:2 * half + 2, :, :]
+            src = pt_t[u][half][:].rearrange("p q t n -> p q n t")
+            if on_vector:
+                nc.vector.tensor_copy(out=dst, in_=src)
+            else:
+                nc.scalar.copy(out=dst, in_=src)
+
+        def quant(u):
+            codes_t[u] = cp.tile([P, JU * P], U32, name="codes", align_bytes=64)
+            scl_t[u] = cp.tile([P, JU * P], U8, name="scl", align_bytes=64)
+            nc.vector.quantize_mx(
+                out=codes_t[u][:].bitcast(FP8X4), scales=scl_t[u][:],
+                in_=grp_t[u][:].rearrange("p j n t -> p (j n t)"),
+            )
+
+        def mx(u):
+            a, j0 = UNITS[u]
+            if u % 2 == 0:
+                po_t[u // 2] = psum_o.tile([P, 2 * JU, B], F32, name="po")
+            po = po_t[u // 2]
+            for jj in range(JU):
+                j = j0 + jj
+                nc.tensor.matmul_mx(
+                    out=po[:, JU * (u % 2) + jj, :],
+                    lhsT=codes_t[u][:, jj * P:(jj + 1) * P].bitcast(FP8X4),
+                    lhsT_scale=scl_t[u][:, jj * P:(jj + 1) * P],
+                    rhs=x_codes[:, j * B:(j + 1) * B].bitcast(FP8X4),
+                    rhs_scale=x_scl[:, j * B:(j + 1) * B],
+                    start=True, stop=True,
+                )
+
+        def evac(u):
+            a, j0 = UNITS[u]
+            if u % UPA == 1:
+                o_t[a] = op.tile([P, B, J], F32, name="o_sb")
+            jb = j0 - JU
+            nc.scalar.copy(
+                out=o_t[a][:, :, jb:jb + 2 * JU], in_=po_t[u // 2][:].rearrange("p j b -> p b j"),
+            )
+            if u % UPA == UPA - 1:
+                nc.sync.dma_start(out=out_v[a], in_=o_t[a][:])
+
+        def at(table, k):
+            return [u for u in range(NU) if table[u] == k]
+
+        xl = 0
+        for u in range(PREFETCH):
+            load(u)
+            if u >= 1:
+                x_load(xl)
+                xl += 1
+        for k in range(max(s_mx[u] for u in range(NU)) + 2):
+            if k + PREFETCH < NU:
+                load(k + PREFETCH)
+            if xl < 8:
+                x_load(xl)
+                xl += 1
+            if 0 <= k - 1 < NU:
+                exps(k - 1)
+            for u in at(s_c, k):
+                copy_out(u, 0, False)
+                if u < C_SPLIT_FROM:
+                    copy_out(u, 1, False)
+            for u in at(s_mx, k - 1):
+                if u % 2 == 1:
+                    evac(u)
+            for u in at(s_n, k):
+                norm(u, False)
+            if 0 <= k - X_STEP < UPA:
+                x_group(k - X_STEP)
+            if k < NU:
+                add_max(k)
+            for u in at(s_c, k):
+                if u >= C_SPLIT_FROM:
+                    copy_out(u, 1, True)
+            for u in at(s_q, k):
+                quant(u)
+            if 0 <= k - X_STEP - 1 < UPA:
+                x_quant(k - X_STEP - 1)
+            if 0 <= k - 1 < NU:
+                recip(k - 1)
+            for u in at(s_n, k):
+                norm(u, True)
+            for u in at(s_n, k):
+                transp(u)
+            for u in at(s_mx, k):
+                mx(u)

@@ -18,69 +18,71 @@ P = 128
 B, N, J = 64, 512, 32
 NT = N // P
 PACK = 4
-JU = 4
-UNITS = [(a, j0) for a in range(NT) for j0 in range(0, J, JU)]
-NU = len(UNITS)
-UPA = J // JU
-
+GJ = 8
+XJ = 4
+FIRST = [1, 1, 2, 4]
+LAST = [4, 2, 1, 1]
 PREFETCH = 6
-X_STEP = 7
-N_ON_V_FROM = 30
-C_SPLIT_FROM = 29
+X_STEP = 5
 
 
-def norm_on_vector(u, jj):
-    return u >= N_ON_V_FROM
+def make_units():
+    units = []
+    for a in range(NT):
+        for g in range(J // GJ):
+            sizes = [4, 4]
+            if a == 0 and g == 0:
+                sizes = FIRST
+            if a == NT - 1 and g == J // GJ - 1:
+                sizes = LAST
+            j0 = g * GJ
+            for nj in sizes:
+                units.append((a, j0, nj))
+                j0 += nj
+    return units
 
 
-def step_tables():
-    s_n, s_c, s_q, s_mx = {}, {}, {}, {}
-    for u in range(NU):
-        s_n[u] = u + 1 if u >= N_ON_V_FROM else u + 2
-        s_c[u] = s_n[u] + 1
-        s_q[u] = s_c[u] + 1
-        early = X_STEP + 3 + u if u < UPA else X_STEP + 3 + UPA + (u - UPA) // 2
-        s_mx[u] = max(s_q[u] + 1, early)
-    return s_n, s_c, s_q, s_mx
+UNITS = make_units()
+NU = len(UNITS)
+
+
+def norm_engine(u, jj):
+    return "S" if jj == 0 else "G"
 
 
 def tile_learnablemasktemporalaggregation_kernel(tc, x, learnable_offset, predefined_weights, out):
     nc = tc.nc
     off_v = learnable_offset.rearrange("j (a p) m -> a p j m", p=P)
-    pre_v = predefined_weights.rearrange("(a p) m -> p a m", p=P)
+    pre_v = predefined_weights.rearrange("(a p) m -> a p m", p=P)
     x_v = x.rearrange("b (p t) j -> p b t j", t=PACK)
     out_v = out.rearrange("b (a p) j -> a p b j", p=P)
-    s_n, s_c, s_q, s_mx = step_tables()
 
     with ExitStack() as ctx:
         const = ctx.enter_context(tc.tile_pool(name="const", bufs=1))
         ld = ctx.enter_context(tc.tile_pool(name="ld", bufs=PREFETCH + 1))
-        zp = ctx.enter_context(tc.tile_pool(name="zp", bufs=4))
+        zp = ctx.enter_context(tc.tile_pool(name="zp", bufs=5))
+        tp = ctx.enter_context(tc.tile_pool(name="tp", bufs=3))
         st = ctx.enter_context(tc.tile_pool(name="st", bufs=6))
         mp = ctx.enter_context(tc.tile_pool(name="mp", bufs=3))
         gp = ctx.enter_context(tc.tile_pool(name="gp", bufs=3))
-        cp = ctx.enter_context(tc.tile_pool(name="cp", bufs=9))
+        cp = ctx.enter_context(tc.tile_pool(name="cp", bufs=5))
         op = ctx.enter_context(tc.tile_pool(name="op", bufs=2))
-        psum_c = ctx.enter_context(tc.psum_pool(name="psum_c", bufs=1))
+        psum_c = ctx.enter_context(tc.psum_pool(name="psum_c", bufs=2))
         psum_t = ctx.enter_context(tc.psum_pool(name="psum_t", bufs=4))
         psum_o = ctx.enter_context(tc.psum_pool(name="psum_o", bufs=2))
         ctx.enter_context(tc.manual_schedule())
 
-        off_t, z_t, nmax_t, ssum_t, rinv_t, mask_t = {}, {}, {}, {}, {}, {}
+        pre_t, off_t, z_t, t1_t, t2_t, nmax_t, ssum_t, rinv_t, mask_t = {}, {}, {}, {}, {}, {}, {}, {}, {}
         pt_t, grp_t, codes_t, scl_t, po_t, o_t = {}, {}, {}, {}, {}, {}
-
-        ident = const.tile([P, P], BF16)
-        make_identity(nc, ident[:])
-        pre_sb = const.tile([P, NT, N], BF16)
-        nc.sync.dma_start(out=pre_sb[:], in_=pre_v)
-        pre_ps = [psum_c.tile([P, 2, N], BF16, name="pre_ps%d" % i) for i in range(2)]
-        for a in range(NT):
-            nc.tensor.matmul(out=pre_ps[a // 2][:, a % 2, :], lhsT=ident[:], rhs=pre_sb[:, a, :], start=True, stop=True)
 
         x_raw = const.tile([P, B * PACK, J], BF16)
         x_grp = const.tile([P, J, B * PACK], BF16, align_bytes=64)
         x_codes = const.tile([P, J * B], U32, align_bytes=64)
         x_scl = const.tile([P, J * B], U8, align_bytes=64)
+        pre_sb = const.tile([P, NT, N], BF16)
+        ident_f = const.tile([P, P], F32)
+        ident_b = const.tile([P, P], BF16)
+        warm = const.tile([P, 1], F32)
 
         def x_load(c):
             nc.sync.dma_start(
@@ -90,100 +92,133 @@ def tile_learnablemasktemporalaggregation_kernel(tc, x, learnable_offset, predef
 
         def x_group(c):
             nc.gpsimd.tensor_scalar(
-                out=x_grp[:, JU * c:JU * (c + 1), :],
-                in0=x_raw[:, :, JU * c:JU * (c + 1)].rearrange("p c j -> p j c"),
+                out=x_grp[:, XJ * c:XJ * (c + 1), :].rearrange("p j (b t) -> p b j t", t=PACK),
+                in0=x_raw[:, :, XJ * c:XJ * (c + 1)].rearrange("p (b t) j -> p b j t", t=PACK),
                 scalar1=1.0, scalar2=0.0, op0=ALU.mult, op1=ALU.add,
             )
 
         def x_quant(c):
-            w = JU * B
+            w = XJ * B
             nc.vector.quantize_mx(
                 out=x_codes[:, w * c:w * (c + 1)].bitcast(FP8X4),
                 scales=x_scl[:, w * c:w * (c + 1)],
-                in_=x_grp[:, JU * c:JU * (c + 1), :].rearrange("p j c -> p (j c)"),
+                in_=x_grp[:, XJ * c:XJ * (c + 1), :].rearrange("p j c -> p (j c)"),
             )
+
+        def load_pre(a):
+            nc.sync.dma_start(out=pre_sb[:, a, :], in_=pre_v[a])
+
+        def pre_to_psum(a):
+            pre_t[a] = psum_c.tile([P, 1, N], BF16, name="pre_ps")
+            nc.tensor.matmul(out=pre_t[a][:, 0, :], lhsT=ident_b[:], rhs=pre_sb[:, a, :], start=True, stop=True)
 
         def load(u):
-            a, j0 = UNITS[u]
-            off_t[u] = ld.tile([P, JU, N], BF16, name="off")
-            nc.sync.dma_start(out=off_t[u][:], in_=off_v[a][:, j0:j0 + JU, :])
+            a, j0, nj = UNITS[u]
+            off_t[u] = ld.tile([P, nj, N], BF16, name="off")
+            nc.sync.dma_start(out=off_t[u][:], in_=off_v[a][:, j0:j0 + nj, :])
 
-        def add_max(u):
-            a, j0 = UNITS[u]
-            z_t[u] = zp.tile([P, JU, N], F32, name="z")
+        def add(u, last):
+            a, j0, nj = UNITS[u]
+            if not last:
+                z_t[u] = zp.tile([P, nj, N], F32, name="z")
+            cut = max(nj - 1, 1)
+            lo, hi = (cut, nj) if last else (0, cut)
+            if lo == hi:
+                return
             nc.vector.tensor_tensor(
-                out=z_t[u][:], in0=off_t[u][:],
-                in1=pre_ps[a // 2][:, a % 2:a % 2 + 1, :].to_broadcast([P, JU, N]), op=ALU.add,
+                out=z_t[u][:, lo:hi, :], in0=off_t[u][:, lo:hi, :],
+                in1=pre_t[a][:].to_broadcast([P, hi - lo, N]), op=ALU.add,
             )
-            nmax_t[u] = st.tile([P, JU], F32, name="nmax")
-            nc.vector.tensor_reduce(out=nmax_t[u][:], in_=z_t[u][:], axis=AX.X, op=ALU.max, negate=True)
+
+        def max1(u):
+            nj = UNITS[u][2]
+            t1_t[u] = tp.tile([P, nj, N // 2], BF16, name="t1")
+            nc.vector.tensor_tensor(
+                out=t1_t[u][:], in0=z_t[u][:, :, 0:N // 2], in1=z_t[u][:, :, N // 2:N], op=ALU.max,
+            )
+
+        def max2(u):
+            nj = UNITS[u][2]
+            t2_t[u] = tp.tile([P, nj, N // 4], BF16, name="t2")
+            nc.vector.tensor_tensor(
+                out=t2_t[u][:], in0=t1_t[u][:, :, 0:N // 4], in1=t1_t[u][:, :, N // 4:N // 2], op=ALU.max,
+            )
+
+        def max3(u):
+            nj = UNITS[u][2]
+            nmax_t[u] = st.tile([P, nj], F32, name="nmax")
+            nc.vector.tensor_reduce(out=nmax_t[u][:], in_=t2_t[u][:], axis=AX.X, op=ALU.max, negate=True)
 
         def exps(u):
-            ssum_t[u] = st.tile([P, JU], F32, name="ssum")
-            for jj in range(JU):
+            nj = UNITS[u][2]
+            ssum_t[u] = st.tile([P, nj], F32, name="ssum")
+            for jj in range(nj):
                 nc.scalar.activation(
                     out=z_t[u][:, jj, :], in_=z_t[u][:, jj, :], func=ACT.Exp,
                     bias=nmax_t[u][:, jj:jj + 1], scale=1.0, accum_out=ssum_t[u][:, jj:jj + 1],
                 )
 
         def recip(u):
-            rinv_t[u] = st.tile([P, JU], F32, name="rinv")
+            nj = UNITS[u][2]
+            rinv_t[u] = st.tile([P, nj], F32, name="rinv")
             nc.vector.reciprocal(out=rinv_t[u][:], in_=ssum_t[u][:])
 
-        def norm(u, on_vector):
+        def norm(u, engine):
+            nj = UNITS[u][2]
             if u not in mask_t:
-                mask_t[u] = mp.tile([P, JU, N], BF16, name="mask")
-            for jj in range(JU):
-                if norm_on_vector(u, jj) != on_vector:
+                mask_t[u] = mp.tile([P, nj, N], BF16, name="mask")
+            for jj in range(nj):
+                if norm_engine(u, jj) != engine:
                     continue
-                if on_vector:
-                    nc.vector.tensor_scalar(
-                        out=mask_t[u][:, jj, :], in0=z_t[u][:, jj, :], scalar1=rinv_t[u][:, jj:jj + 1],
-                        scalar2=None, op0=ALU.mult,
-                    )
+                dst, src, r = mask_t[u][:, jj, :], z_t[u][:, jj, :], rinv_t[u][:, jj:jj + 1]
+                if engine == "V":
+                    nc.vector.tensor_scalar(out=dst, in0=src, scalar1=r, scalar2=None, op0=ALU.mult)
+                elif engine == "S":
+                    nc.scalar.activation(out=dst, in_=src, func=ACT.Copy, scale=r)
                 else:
-                    nc.gpsimd.tensor_scalar(
-                        out=mask_t[u][:, jj, :], in0=z_t[u][:, jj, :], scalar1=rinv_t[u][:, jj:jj + 1],
-                        scalar2=0.0, op0=ALU.mult, op1=ALU.add,
-                    )
+                    nc.gpsimd.tensor_scalar(out=dst, in0=src, scalar1=r, scalar2=0.0, op0=ALU.mult, op1=ALU.add)
 
         def transp(u):
+            nj = UNITS[u][2]
             pt_t[u] = []
-            for half in range(2):
-                pt = psum_t.tile([P, 2, PACK, P], BF16, name="pt")
+            words = mask_t[u][:].rearrange("p j m -> p (j m)").bitcast(F32)
+            for j0 in range(0, nj, 2):
+                pt = psum_t.tile([P, 2, 2, P], F32, name="pt")
                 pt_t[u].append(pt)
-                for q in range(2):
-                    jj = 2 * half + q
-                    for t in range(PACK):
-                        nc.tensor.transpose(pt[:, q, t, :], mask_t[u][:, jj, t:N:PACK], ident[:])
+                for jj in range(j0, min(j0 + 2, nj)):
+                    for e in range(2):
+                        w0 = jj * (N // 2) + e
+                        nc.tensor.transpose(pt[:, jj - j0, e, :], words[:, w0:w0 + N // 2 - 1:2], ident_f[:])
 
-        def copy_out(u, half, on_vector):
-            if u not in grp_t:
-                grp_t[u] = gp.tile([P, JU, P, PACK], BF16, name="grp", align_bytes=64)
-            dst = grp_t[u][:, 2 * half:2 * half + 2, :, :]
-            src = pt_t[u][half][:].rearrange("p q t n -> p q n t")
-            if on_vector:
-                nc.vector.tensor_copy(out=dst, in_=src)
-            else:
-                nc.scalar.copy(out=dst, in_=src)
+        def copy_out(u):
+            nj = UNITS[u][2]
+            grp_t[u] = gp.tile([P, nj, P, PACK], BF16, name="grp", align_bytes=64)
+            words = grp_t[u][:].rearrange("p j n t -> p (j n t)").bitcast(F32)
+            for i, pt in enumerate(pt_t[u]):
+                q = min(2, nj - 2 * i)
+                nc.scalar.copy(
+                    out=words[:, 2 * i * 2 * P:(2 * i + q) * 2 * P].rearrange("p (q n e) -> p q n e", q=q, e=2),
+                    in_=pt[:, 0:q, :, :].rearrange("p q e n -> p q n e"),
+                )
 
         def quant(u):
-            codes_t[u] = cp.tile([P, JU * P], U32, name="codes", align_bytes=64)
-            scl_t[u] = cp.tile([P, JU * P], U8, name="scl", align_bytes=64)
+            nj = UNITS[u][2]
+            codes_t[u] = cp.tile([P, nj * P], U32, name="codes", align_bytes=64)
+            scl_t[u] = cp.tile([P, nj * P], U8, name="scl", align_bytes=64)
             nc.vector.quantize_mx(
                 out=codes_t[u][:].bitcast(FP8X4), scales=scl_t[u][:],
                 in_=grp_t[u][:].rearrange("p j n t -> p (j n t)"),
             )
 
         def mx(u):
-            a, j0 = UNITS[u]
-            if u % 2 == 0:
-                po_t[u // 2] = psum_o.tile([P, 2 * JU, B], F32, name="po")
-            po = po_t[u // 2]
-            for jj in range(JU):
+            a, j0, nj = UNITS[u]
+            g = (a, j0 // GJ)
+            if j0 % GJ == 0:
+                po_t[g] = psum_o.tile([P, GJ, B], F32, name="po")
+            for jj in range(nj):
                 j = j0 + jj
                 nc.tensor.matmul_mx(
-                    out=po[:, JU * (u % 2) + jj, :],
+                    out=po_t[g][:, j % GJ, :],
                     lhsT=codes_t[u][:, jj * P:(jj + 1) * P].bitcast(FP8X4),
                     lhsT_scale=scl_t[u][:, jj * P:(jj + 1) * P],
                     rhs=x_codes[:, j * B:(j + 1) * B].bitcast(FP8X4),
@@ -192,58 +227,77 @@ def tile_learnablemasktemporalaggregation_kernel(tc, x, learnable_offset, predef
                 )
 
         def evac(u):
-            a, j0 = UNITS[u]
-            if u % UPA == 1:
+            a, j0, nj = UNITS[u]
+            if (j0 + nj) % GJ != 0:
+                return
+            g = j0 // GJ
+            if g == 0:
                 o_t[a] = op.tile([P, B, J], F32, name="o_sb")
-            jb = j0 - JU
             nc.scalar.copy(
-                out=o_t[a][:, :, jb:jb + 2 * JU], in_=po_t[u // 2][:].rearrange("p j b -> p b j"),
+                out=o_t[a][:, :, GJ * g:GJ * (g + 1)], in_=po_t[(a, g)][:].rearrange("p j b -> p b j"),
             )
-            if u % UPA == UPA - 1:
-                nc.sync.dma_start(out=out_v[a], in_=o_t[a][:])
+            if a < NT - 1:
+                if g == J // GJ - 1:
+                    nc.sync.dma_start(out=out_v[a], in_=o_t[a][:])
+            elif g == 1:
+                nc.sync.dma_start(out=out_v[a][:, :, 0:2 * GJ], in_=o_t[a][:, :, 0:2 * GJ])
+            elif g > 1:
+                nc.sync.dma_start(out=out_v[a][:, :, GJ * g:GJ * (g + 1)], in_=o_t[a][:, :, GJ * g:GJ * (g + 1)])
 
-        def at(table, k):
-            return [u for u in range(NU) if table[u] == k]
+        nc.vector.memset(warm[:], 0.0)
+        nc.scalar.activation(out=warm[:], in_=warm[:], func=ACT.Exp)
+        make_identity(nc, ident_f[:])
+        nc.vector.tensor_copy(out=ident_b[:], in_=ident_f[:])
+        load_pre(0)
+        load(0)
+        load(1)
+        load(2)
+        pre_to_psum(0)
+        for c in range(4):
+            x_load(c)
+        load(3)
+        for c in range(4, 8):
+            x_load(c)
+        load(4)
+        load(5)
+        for a in range(1, NT):
+            load_pre(a)
 
-        xl = 0
-        for u in range(PREFETCH):
-            load(u)
-            if u >= 1:
-                x_load(xl)
-                xl += 1
-        for k in range(max(s_mx[u] for u in range(NU)) + 2):
+        for k in range(NU + 7):
             if k + PREFETCH < NU:
                 load(k + PREFETCH)
-            if xl < 8:
-                x_load(xl)
-                xl += 1
-            if 0 <= k - 1 < NU:
-                exps(k - 1)
-            for u in at(s_c, k):
-                copy_out(u, 0, False)
-                if u < C_SPLIT_FROM:
-                    copy_out(u, 1, False)
-            for u in at(s_mx, k - 1):
-                if u % 2 == 1:
-                    evac(u)
-            for u in at(s_n, k):
-                norm(u, False)
-            if 0 <= k - X_STEP < UPA:
-                x_group(k - X_STEP)
+            if 0 <= k - 2 < NU:
+                exps(k - 2)
+            if 0 <= k - 3 < NU:
+                recip(k - 3)
+            if 0 <= k - 4 < NU:
+                copy_out(k - 4)
+            if 0 <= k - 3 < NU:
+                norm(k - 3, "S")
+                norm(k - 3, "G")
             if k < NU:
-                add_max(k)
-            for u in at(s_c, k):
-                if u >= C_SPLIT_FROM:
-                    copy_out(u, 1, True)
-            for u in at(s_q, k):
-                quant(u)
-            if 0 <= k - X_STEP - 1 < UPA:
-                x_quant(k - X_STEP - 1)
+                add(k, False)
             if 0 <= k - 1 < NU:
-                recip(k - 1)
-            for u in at(s_n, k):
-                norm(u, True)
-            for u in at(s_n, k):
-                transp(u)
-            for u in at(s_mx, k):
-                mx(u)
+                max1(k - 1)
+            if 0 <= k - 5 < NU:
+                quant(k - 5)
+            if 0 <= k - X_STEP < J // XJ:
+                x_group(k - X_STEP)
+            if 0 <= k - 1 < NU:
+                max2(k - 1)
+            if k < NU:
+                add(k, True)
+            if 0 <= k - X_STEP - 1 < J // XJ:
+                x_quant(k - X_STEP - 1)
+            if 0 <= k - 3 < NU:
+                norm(k - 3, "V")
+            if 0 <= k - 1 < NU:
+                max3(k - 1)
+            if 0 <= k - 7 < NU:
+                evac(k - 7)
+            if 4 <= k < NU + 4 and (k == 4 or UNITS[k - 4][0] != UNITS[k - 5][0]) and UNITS[k - 4][0] < NT - 1:
+                pre_to_psum(UNITS[k - 4][0] + 1)
+            if 0 <= k - 6 < NU:
+                mx(k - 6)
+            if 0 <= k - 3 < NU:
+                transp(k - 3)

@@ -20,10 +20,15 @@ NT = N // P
 PACK = 4
 GJ = 8
 XJ = 4
-FIRST = [1, 1, 2, 4]
-LAST = [4, 2, 1, 1]
+FIRST = [4, 4]
+LAST = [2, 2, 2, 2]
 PREFETCH = 6
 X_STEP = 5
+N_EARLY = 10
+N_LATE = 4
+PAT = "SGGG"
+PAT_EARLY = "SSGG"
+PAT_LATE = "GVGV"
 
 
 def make_units():
@@ -47,7 +52,11 @@ NU = len(UNITS)
 
 
 def norm_engine(u, jj):
-    return "S" if jj == 0 else "G"
+    if u < N_EARLY:
+        return PAT_EARLY[jj]
+    if u >= NU - N_LATE:
+        return PAT_LATE[jj]
+    return PAT[jj]
 
 
 def tile_learnablemasktemporalaggregation_kernel(tc, x, learnable_offset, predefined_weights, out):
@@ -72,7 +81,7 @@ def tile_learnablemasktemporalaggregation_kernel(tc, x, learnable_offset, predef
         psum_o = ctx.enter_context(tc.psum_pool(name="psum_o", bufs=2))
         ctx.enter_context(tc.manual_schedule())
 
-        pre_t, off_t, z_t, t1_t, t2_t, nmax_t, ssum_t, rinv_t, mask_t = {}, {}, {}, {}, {}, {}, {}, {}, {}
+        pre_t, off_t, z_t, t1_t, t2_t, t3_t, nmax_t, ssum_t, rinv_t, mask_t = {}, {}, {}, {}, {}, {}, {}, {}, {}, {}
         pt_t, grp_t, codes_t, scl_t, po_t, o_t = {}, {}, {}, {}, {}, {}
 
         x_raw = const.tile([P, B * PACK, J], BF16)
@@ -117,13 +126,11 @@ def tile_learnablemasktemporalaggregation_kernel(tc, x, learnable_offset, predef
             off_t[u] = ld.tile([P, nj, N], BF16, name="off")
             nc.sync.dma_start(out=off_t[u][:], in_=off_v[a][:, j0:j0 + nj, :])
 
-        def add(u, last):
+        def add(u, lo, hi):
             a, j0, nj = UNITS[u]
-            if not last:
+            if lo == 0:
                 z_t[u] = zp.tile([P, nj, N], F32, name="z")
-            cut = max(nj - 1, 1)
-            lo, hi = (cut, nj) if last else (0, cut)
-            if lo == hi:
+            if lo >= hi:
                 return
             nc.vector.tensor_tensor(
                 out=z_t[u][:, lo:hi, :], in0=off_t[u][:, lo:hi, :],
@@ -146,8 +153,16 @@ def tile_learnablemasktemporalaggregation_kernel(tc, x, learnable_offset, predef
 
         def max3(u):
             nj = UNITS[u][2]
+            t3_t[u] = tp.tile([P, nj, N // 8], BF16, name="t3")
+            nc.vector.tensor_tensor(
+                out=t3_t[u][:], in0=t2_t[u][:, :, 0:N // 8], in1=t2_t[u][:, :, N // 8:N // 4], op=ALU.max,
+            )
+
+        def max_last(u):
+            nj = UNITS[u][2]
             nmax_t[u] = st.tile([P, nj], F32, name="nmax")
-            nc.vector.tensor_reduce(out=nmax_t[u][:], in_=t2_t[u][:], axis=AX.X, op=ALU.max, negate=True)
+            t = t3_t[u] if u in t3_t else t2_t[u]
+            nc.vector.tensor_reduce(out=nmax_t[u][:], in_=t[:], axis=AX.X, op=ALU.max, negate=True)
 
         def exps(u):
             nj = UNITS[u][2]
@@ -196,10 +211,9 @@ def tile_learnablemasktemporalaggregation_kernel(tc, x, learnable_offset, predef
             words = grp_t[u][:].rearrange("p j n t -> p (j n t)").bitcast(F32)
             for i, pt in enumerate(pt_t[u]):
                 q = min(2, nj - 2 * i)
-                nc.scalar.copy(
-                    out=words[:, 2 * i * 2 * P:(2 * i + q) * 2 * P].rearrange("p (q n e) -> p q n e", q=q, e=2),
-                    in_=pt[:, 0:q, :, :].rearrange("p q e n -> p q n e"),
-                )
+                dst = words[:, 2 * i * 2 * P:(2 * i + q) * 2 * P].rearrange("p (q n e) -> p q n e", q=q, e=2)
+                src = pt[:, 0:q, :, :].rearrange("p q e n -> p q n e")
+                nc.scalar.copy(out=dst, in_=src)
 
         def quant(u):
             nj = UNITS[u][2]
@@ -264,19 +278,18 @@ def tile_learnablemasktemporalaggregation_kernel(tc, x, learnable_offset, predef
             load_pre(a)
 
         for k in range(NU + 7):
+            nk = UNITS[k][2] if k < NU else 0
+            cut = max(nk - 1, 1)
             if k + PREFETCH < NU:
                 load(k + PREFETCH)
             if 0 <= k - 2 < NU:
                 exps(k - 2)
             if 0 <= k - 3 < NU:
-                recip(k - 3)
+                norm(k - 3, "S")
             if 0 <= k - 4 < NU:
                 copy_out(k - 4)
-            if 0 <= k - 3 < NU:
-                norm(k - 3, "S")
-                norm(k - 3, "G")
             if k < NU:
-                add(k, False)
+                add(k, 0, cut)
             if 0 <= k - 1 < NU:
                 max1(k - 1)
             if 0 <= k - 5 < NU:
@@ -285,14 +298,19 @@ def tile_learnablemasktemporalaggregation_kernel(tc, x, learnable_offset, predef
                 x_group(k - X_STEP)
             if 0 <= k - 1 < NU:
                 max2(k - 1)
-            if k < NU:
-                add(k, True)
             if 0 <= k - X_STEP - 1 < J // XJ:
                 x_quant(k - X_STEP - 1)
             if 0 <= k - 3 < NU:
                 norm(k - 3, "V")
+            if 0 <= k - 2 < NU:
+                recip(k - 2)
+                norm(k - 2, "G")
             if 0 <= k - 1 < NU:
                 max3(k - 1)
+            if k < NU:
+                add(k, cut, nk)
+            if 0 <= k - 1 < NU:
+                max_last(k - 1)
             if 0 <= k - 7 < NU:
                 evac(k - 7)
             if 4 <= k < NU + 4 and (k == 4 or UNITS[k - 4][0] != UNITS[k - 5][0]) and UNITS[k - 4][0] < NT - 1:

@@ -20,15 +20,17 @@ NT = N // P
 PACK = 4
 GJ = 8
 XJ = 4
-FIRST = [4, 4]
-LAST = [2, 2, 2, 2]
+FIRST = [1, 1, 2, 4]
+LAST = [4, 2, 1, 1]
 PREFETCH = 6
-X_STEP = 5
-N_EARLY = 10
-N_LATE = 4
+X_STEP = 4
+MX_START = 6
+N_EARLY = X_STEP + J // XJ - 1
+N_LATE = 3
 PAT = "SGGG"
 PAT_EARLY = "SSGG"
-PAT_LATE = "GVGV"
+PAT_LATE = "VSVG"
+GADD = {1: 0, 2: 1, 4: 1}
 
 
 def make_units():
@@ -51,6 +53,10 @@ UNITS = make_units()
 NU = len(UNITS)
 
 
+def g_adds(u):
+    return GADD[UNITS[u][2]]
+
+
 def norm_engine(u, jj):
     if u < N_EARLY:
         return PAT_EARLY[jj]
@@ -69,8 +75,7 @@ def tile_learnablemasktemporalaggregation_kernel(tc, x, learnable_offset, predef
     with ExitStack() as ctx:
         const = ctx.enter_context(tc.tile_pool(name="const", bufs=1))
         ld = ctx.enter_context(tc.tile_pool(name="ld", bufs=PREFETCH + 1))
-        zp = ctx.enter_context(tc.tile_pool(name="zp", bufs=5))
-        tp = ctx.enter_context(tc.tile_pool(name="tp", bufs=3))
+        zp = ctx.enter_context(tc.tile_pool(name="zp", bufs=6))
         st = ctx.enter_context(tc.tile_pool(name="st", bufs=6))
         mp = ctx.enter_context(tc.tile_pool(name="mp", bufs=3))
         gp = ctx.enter_context(tc.tile_pool(name="gp", bufs=3))
@@ -81,7 +86,7 @@ def tile_learnablemasktemporalaggregation_kernel(tc, x, learnable_offset, predef
         psum_o = ctx.enter_context(tc.psum_pool(name="psum_o", bufs=2))
         ctx.enter_context(tc.manual_schedule())
 
-        pre_t, off_t, z_t, t1_t, t2_t, t3_t, nmax_t, ssum_t, rinv_t, mask_t = {}, {}, {}, {}, {}, {}, {}, {}, {}, {}
+        pre_t, off_t, z_t, nmax_t, ssum_t, rinv_t, mask_t = {}, {}, {}, {}, {}, {}, {}
         pt_t, grp_t, codes_t, scl_t, po_t, o_t = {}, {}, {}, {}, {}, {}
 
         x_raw = const.tile([P, B * PACK, J], BF16)
@@ -126,43 +131,38 @@ def tile_learnablemasktemporalaggregation_kernel(tc, x, learnable_offset, predef
             off_t[u] = ld.tile([P, nj, N], BF16, name="off")
             nc.sync.dma_start(out=off_t[u][:], in_=off_v[a][:, j0:j0 + nj, :])
 
+        def new_z(u):
+            z_t[u] = zp.tile([P, UNITS[u][2], N], F32, name="z")
+
+        def half(u):
+            return UNITS[u][2] // 2
+
         def add(u, lo, hi):
-            a, j0, nj = UNITS[u]
-            if lo == 0:
-                z_t[u] = zp.tile([P, nj, N], F32, name="z")
+            if u not in z_t:
+                new_z(u)
             if lo >= hi:
                 return
             nc.vector.tensor_tensor(
                 out=z_t[u][:, lo:hi, :], in0=off_t[u][:, lo:hi, :],
-                in1=pre_t[a][:].to_broadcast([P, hi - lo, N]), op=ALU.add,
+                in1=pre_t[UNITS[u][0]][:].to_broadcast([P, hi - lo, N]), op=ALU.add,
             )
 
-        def max1(u):
-            nj = UNITS[u][2]
-            t1_t[u] = tp.tile([P, nj, N // 2], BF16, name="t1")
-            nc.vector.tensor_tensor(
-                out=t1_t[u][:], in0=z_t[u][:, :, 0:N // 2], in1=z_t[u][:, :, N // 2:N], op=ALU.max,
-            )
+        def add_gpsimd(u):
+            a, j0, nj = UNITS[u]
+            new_z(u)
+            for jj in range(nj - g_adds(u), nj):
+                nc.gpsimd.tensor_tensor(
+                    out=z_t[u][:, jj, :], in0=off_t[u][:, jj, :], in1=pre_sb[:, a, :], op=ALU.add,
+                )
 
-        def max2(u):
-            nj = UNITS[u][2]
-            t2_t[u] = tp.tile([P, nj, N // 4], BF16, name="t2")
-            nc.vector.tensor_tensor(
-                out=t2_t[u][:], in0=t1_t[u][:, :, 0:N // 4], in1=t1_t[u][:, :, N // 4:N // 2], op=ALU.max,
+        def row_max(u, lo, hi):
+            if u not in nmax_t:
+                nmax_t[u] = st.tile([P, UNITS[u][2]], F32, name="nmax")
+            if lo >= hi:
+                return
+            nc.vector.tensor_reduce(
+                out=nmax_t[u][:, lo:hi], in_=z_t[u][:, lo:hi, :], axis=AX.X, op=ALU.max, negate=True,
             )
-
-        def max3(u):
-            nj = UNITS[u][2]
-            t3_t[u] = tp.tile([P, nj, N // 8], BF16, name="t3")
-            nc.vector.tensor_tensor(
-                out=t3_t[u][:], in0=t2_t[u][:, :, 0:N // 8], in1=t2_t[u][:, :, N // 8:N // 4], op=ALU.max,
-            )
-
-        def max_last(u):
-            nj = UNITS[u][2]
-            nmax_t[u] = st.tile([P, nj], F32, name="nmax")
-            t = t3_t[u] if u in t3_t else t2_t[u]
-            nc.vector.tensor_reduce(out=nmax_t[u][:], in_=t[:], axis=AX.X, op=ALU.max, negate=True)
 
         def exps(u):
             nj = UNITS[u][2]
@@ -253,10 +253,8 @@ def tile_learnablemasktemporalaggregation_kernel(tc, x, learnable_offset, predef
             if a < NT - 1:
                 if g == J // GJ - 1:
                     nc.sync.dma_start(out=out_v[a], in_=o_t[a][:])
-            elif g == 1:
-                nc.sync.dma_start(out=out_v[a][:, :, 0:2 * GJ], in_=o_t[a][:, :, 0:2 * GJ])
-            elif g > 1:
-                nc.sync.dma_start(out=out_v[a][:, :, GJ * g:GJ * (g + 1)], in_=o_t[a][:, :, GJ * g:GJ * (g + 1)])
+            elif g % 2 == 1:
+                nc.sync.dma_start(out=out_v[a][:, :, GJ * (g - 1):GJ * (g + 1)], in_=o_t[a][:, :, GJ * (g - 1):GJ * (g + 1)])
 
         nc.vector.memset(warm[:], 0.0)
         nc.scalar.activation(out=warm[:], in_=warm[:], func=ACT.Exp)
@@ -267,55 +265,53 @@ def tile_learnablemasktemporalaggregation_kernel(tc, x, learnable_offset, predef
         load(1)
         load(2)
         pre_to_psum(0)
-        for c in range(4):
-            x_load(c)
         load(3)
-        for c in range(4, 8):
-            x_load(c)
+        x_load(0)
+        x_load(1)
         load(4)
+        for c in range(2, 6):
+            x_load(c)
         load(5)
+        x_load(6)
+        x_load(7)
         for a in range(1, NT):
             load_pre(a)
 
-        for k in range(NU + 7):
-            nk = UNITS[k][2] if k < NU else 0
-            cut = max(nk - 1, 1)
-            if k + PREFETCH < NU:
+        for k in range(-1, NU + 5):
+            if 0 <= k and k + PREFETCH < NU:
                 load(k + PREFETCH)
-            if 0 <= k - 2 < NU:
-                exps(k - 2)
-            if 0 <= k - 3 < NU:
-                norm(k - 3, "S")
-            if 0 <= k - 4 < NU:
-                copy_out(k - 4)
-            if k < NU:
-                add(k, 0, cut)
             if 0 <= k - 1 < NU:
-                max1(k - 1)
-            if 0 <= k - 5 < NU:
-                quant(k - 5)
+                exps(k - 1)
+            if 0 <= k < NU:
+                add(k, 0, half(k))
+                add(k, half(k), UNITS[k][2] - g_adds(k))
+                row_max(k, 0, half(k))
+            if 0 <= k - 3 < NU:
+                quant(k - 3)
+            if 0 <= k - 1 < NU:
+                recip(k - 1)
+                norm(k - 1, "V")
+                norm(k - 1, "G")
+            if 0 <= k - 2 < NU:
+                copy_out(k - 2)
+            if 0 <= k - 1 < NU:
+                norm(k - 1, "S")
+            if k + 1 < NU:
+                add_gpsimd(k + 1)
             if 0 <= k - X_STEP < J // XJ:
                 x_group(k - X_STEP)
-            if 0 <= k - 1 < NU:
-                max2(k - 1)
             if 0 <= k - X_STEP - 1 < J // XJ:
                 x_quant(k - X_STEP - 1)
-            if 0 <= k - 3 < NU:
-                norm(k - 3, "V")
-            if 0 <= k - 2 < NU:
-                recip(k - 2)
-                norm(k - 2, "G")
-            if 0 <= k - 1 < NU:
-                max3(k - 1)
-            if k < NU:
-                add(k, cut, nk)
-            if 0 <= k - 1 < NU:
-                max_last(k - 1)
-            if 0 <= k - 7 < NU:
-                evac(k - 7)
+            if 0 <= k < NU:
+                row_max(k, half(k), UNITS[k][2])
             if 4 <= k < NU + 4 and (k == 4 or UNITS[k - 4][0] != UNITS[k - 5][0]) and UNITS[k - 4][0] < NT - 1:
                 pre_to_psum(UNITS[k - 4][0] + 1)
-            if 0 <= k - 6 < NU:
-                mx(k - 6)
-            if 0 <= k - 3 < NU:
-                transp(k - 3)
+            if k == MX_START:
+                for u in range(MX_START - 4):
+                    mx(u)
+            if k >= MX_START and k - 4 < NU:
+                mx(k - 4)
+            if 0 <= k - 4 < NU:
+                evac(k - 4)
+            if 0 <= k - 1 < NU:
+                transp(k - 1)

@@ -22,24 +22,22 @@ GJ = 8
 XJ = 4
 FIRST = [1, 1, 2, 4]
 LAST = [4, 2, 1, 1]
-PREFETCH = 6
-X_STEP = 4
+PREFETCH = 4
 MX_START = 6
-N_EARLY = X_STEP + J // XJ - 1
+X_STEP = 4
+N_EARLY = X_STEP + J // (2 * XJ) - 1
 N_LATE = 3
-PAT = "SGGG"
-PAT_EARLY = "SSGG"
-PAT_LATE = "VSVG"
-GADD = {1: 0, 2: 1, 4: 1}
 
 
 def make_units():
     units = []
     for a in range(NT):
         for g in range(J // GJ):
-            sizes = [4, 4]
+            sizes = [8]
             if a == 0 and g == 0:
                 sizes = FIRST
+            if a == NT - 1 and g == J // GJ - 2:
+                sizes = [4, 4]
             if a == NT - 1 and g == J // GJ - 1:
                 sizes = LAST
             j0 = g * GJ
@@ -54,15 +52,17 @@ NU = len(UNITS)
 
 
 def g_adds(u):
-    return GADD[UNITS[u][2]]
+    nj = UNITS[u][2]
+    return nj // 4 if nj > 2 else nj // 2
 
 
 def norm_engine(u, jj):
-    if u < N_EARLY:
-        return PAT_EARLY[jj]
+    nj = UNITS[u][2]
     if u >= NU - N_LATE:
-        return PAT_LATE[jj]
-    return PAT[jj]
+        return "VS"[jj % 2]
+    if u < N_EARLY:
+        return "S" if 2 * jj < nj else "G"
+    return "S" if 4 * jj < nj else "G"
 
 
 def tile_learnablemasktemporalaggregation_kernel(tc, x, learnable_offset, predefined_weights, out):
@@ -75,11 +75,11 @@ def tile_learnablemasktemporalaggregation_kernel(tc, x, learnable_offset, predef
     with ExitStack() as ctx:
         const = ctx.enter_context(tc.tile_pool(name="const", bufs=1))
         ld = ctx.enter_context(tc.tile_pool(name="ld", bufs=PREFETCH + 1))
-        zp = ctx.enter_context(tc.tile_pool(name="zp", bufs=6))
+        zp = ctx.enter_context(tc.tile_pool(name="zp", bufs=4))
         st = ctx.enter_context(tc.tile_pool(name="st", bufs=6))
         mp = ctx.enter_context(tc.tile_pool(name="mp", bufs=3))
-        gp = ctx.enter_context(tc.tile_pool(name="gp", bufs=3))
-        cp = ctx.enter_context(tc.tile_pool(name="cp", bufs=5))
+        gp = ctx.enter_context(tc.tile_pool(name="gp", bufs=2))
+        cp = ctx.enter_context(tc.tile_pool(name="cp", bufs=4))
         op = ctx.enter_context(tc.tile_pool(name="op", bufs=2))
         psum_c = ctx.enter_context(tc.psum_pool(name="psum_c", bufs=2))
         psum_t = ctx.enter_context(tc.psum_pool(name="psum_t", bufs=4))
@@ -112,11 +112,11 @@ def tile_learnablemasktemporalaggregation_kernel(tc, x, learnable_offset, predef
             )
 
         def x_quant(c):
-            w = XJ * B
+            w = 2 * XJ * B
             nc.vector.quantize_mx(
                 out=x_codes[:, w * c:w * (c + 1)].bitcast(FP8X4),
                 scales=x_scl[:, w * c:w * (c + 1)],
-                in_=x_grp[:, XJ * c:XJ * (c + 1), :].rearrange("p j c -> p (j c)"),
+                in_=x_grp[:, 2 * XJ * c:2 * XJ * (c + 1), :].rearrange("p j c -> p (j c)"),
             )
 
         def load_pre(a):
@@ -164,10 +164,10 @@ def tile_learnablemasktemporalaggregation_kernel(tc, x, learnable_offset, predef
                 out=nmax_t[u][:, lo:hi], in_=z_t[u][:, lo:hi, :], axis=AX.X, op=ALU.max, negate=True,
             )
 
-        def exps(u):
-            nj = UNITS[u][2]
-            ssum_t[u] = st.tile([P, nj], F32, name="ssum")
-            for jj in range(nj):
+        def exps(u, lo, hi):
+            if u not in ssum_t:
+                ssum_t[u] = st.tile([P, UNITS[u][2]], F32, name="ssum")
+            for jj in range(lo, hi):
                 nc.scalar.activation(
                     out=z_t[u][:, jj, :], in_=z_t[u][:, jj, :], func=ACT.Exp,
                     bias=nmax_t[u][:, jj:jj + 1], scale=1.0, accum_out=ssum_t[u][:, jj:jj + 1],
@@ -261,31 +261,27 @@ def tile_learnablemasktemporalaggregation_kernel(tc, x, learnable_offset, predef
         make_identity(nc, ident_f[:])
         nc.vector.tensor_copy(out=ident_b[:], in_=ident_f[:])
         load_pre(0)
-        load(0)
-        load(1)
-        load(2)
+        for u in range(4):
+            load(u)
         pre_to_psum(0)
-        load(3)
-        x_load(0)
-        x_load(1)
+        for c in range(2):
+            x_load(c)
         load(4)
         for c in range(2, 6):
             x_load(c)
         load(5)
-        x_load(6)
-        x_load(7)
+        for c in range(6, 8):
+            x_load(c)
         for a in range(1, NT):
             load_pre(a)
 
         for k in range(-1, NU + 5):
-            if 0 <= k and k + PREFETCH < NU:
+            if 6 <= k + PREFETCH < NU:
                 load(k + PREFETCH)
             if 0 <= k - 1 < NU:
-                exps(k - 1)
+                exps(k - 1, half(k - 1), UNITS[k - 1][2])
             if 0 <= k < NU:
-                add(k, 0, half(k))
-                add(k, half(k), UNITS[k][2] - g_adds(k))
-                row_max(k, 0, half(k))
+                add(k, 0, UNITS[k][2] - g_adds(k))
             if 0 <= k - 3 < NU:
                 quant(k - 3)
             if 0 <= k - 1 < NU:
@@ -298,14 +294,16 @@ def tile_learnablemasktemporalaggregation_kernel(tc, x, learnable_offset, predef
                 norm(k - 1, "S")
             if k + 1 < NU:
                 add_gpsimd(k + 1)
-            if 0 <= k - X_STEP < J // XJ:
-                x_group(k - X_STEP)
-            if 0 <= k - X_STEP - 1 < J // XJ:
+            if 0 <= k - X_STEP < J // (2 * XJ):
+                x_group(2 * (k - X_STEP))
+                x_group(2 * (k - X_STEP) + 1)
+            if 0 <= k - X_STEP - 1 < J // (2 * XJ):
                 x_quant(k - X_STEP - 1)
             if 0 <= k < NU:
+                row_max(k, 0, half(k))
                 row_max(k, half(k), UNITS[k][2])
-            if 4 <= k < NU + 4 and (k == 4 or UNITS[k - 4][0] != UNITS[k - 5][0]) and UNITS[k - 4][0] < NT - 1:
-                pre_to_psum(UNITS[k - 4][0] + 1)
+            if 0 <= k < NU - 2 and UNITS[k + 2][0] != UNITS[k + 1][0]:
+                pre_to_psum(UNITS[k + 2][0])
             if k == MX_START:
                 for u in range(MX_START - 4):
                     mx(u)
@@ -313,5 +311,7 @@ def tile_learnablemasktemporalaggregation_kernel(tc, x, learnable_offset, predef
                 mx(k - 4)
             if 0 <= k - 4 < NU:
                 evac(k - 4)
+            if 0 <= k < NU:
+                exps(k, 0, half(k))
             if 0 <= k - 1 < NU:
                 transp(k - 1)

@@ -53,6 +53,8 @@ NU = len(UNITS)
 
 def g_adds(u):
     nj = UNITS[u][2]
+    if 2 <= u < len(FIRST) + 1:
+        return -(-nj // 3)
     return nj // 4 if nj > 2 else nj // 2
 
 
@@ -142,17 +144,21 @@ def tile_learnablemasktemporalaggregation_kernel(tc, x, learnable_offset, predef
                 new_z(u)
             if lo >= hi:
                 return
+            a = UNITS[u][0]
+            pre = pre_sb[:, a:a + 1, :] if u == 0 else pre_t[a][:]
             nc.vector.tensor_tensor(
                 out=z_t[u][:, lo:hi, :], in0=off_t[u][:, lo:hi, :],
-                in1=pre_t[UNITS[u][0]][:].to_broadcast([P, hi - lo, N]), op=ALU.add,
+                in1=pre.to_broadcast([P, hi - lo, N]), op=ALU.add,
             )
 
         def add_gpsimd(u):
             a, j0, nj = UNITS[u]
             new_z(u)
-            for jj in range(nj - g_adds(u), nj):
+            n = g_adds(u)
+            if n > 0:
                 nc.gpsimd.tensor_tensor(
-                    out=z_t[u][:, jj, :], in0=off_t[u][:, jj, :], in1=pre_sb[:, a, :], op=ALU.add,
+                    out=z_t[u][:, nj - n:nj, :], in0=off_t[u][:, nj - n:nj, :],
+                    in1=pre_sb[:, a:a + 1, :].to_broadcast([P, n, N]), op=ALU.add,
                 )
 
         def row_max(u, lo, hi):
@@ -247,14 +253,24 @@ def tile_learnablemasktemporalaggregation_kernel(tc, x, learnable_offset, predef
             g = j0 // GJ
             if g == 0:
                 o_t[a] = op.tile([P, B, J], F32, name="o_sb")
-            nc.scalar.copy(
-                out=o_t[a][:, :, GJ * g:GJ * (g + 1)], in_=po_t[(a, g)][:].rearrange("p j b -> p b j"),
-            )
+            last = a == NT - 1 and g == J // GJ - 1
+            parts = [(0, B // 2, nc.sync), (B // 2, B, nc.scalar)] if last else [(0, B, nc.sync)]
+            for lo, hi, queue in parts:
+                nc.scalar.copy(
+                    out=o_t[a][:, lo:hi, GJ * g:GJ * (g + 1)],
+                    in_=po_t[(a, g)][:, :, lo:hi].rearrange("p j b -> p b j"),
+                )
+                if last:
+                    queue.dma_start(out=out_v[a][:, lo:hi, GJ * g:], in_=o_t[a][:, lo:hi, GJ * g:])
+            if last:
+                return
             if a < NT - 1:
                 if g == J // GJ - 1:
                     nc.sync.dma_start(out=out_v[a], in_=o_t[a][:])
-            elif g % 2 == 1:
-                nc.sync.dma_start(out=out_v[a][:, :, GJ * (g - 1):GJ * (g + 1)], in_=o_t[a][:, :, GJ * (g - 1):GJ * (g + 1)])
+            elif g == 1:
+                nc.sync.dma_start(out=out_v[a][:, :, 0:2 * GJ], in_=o_t[a][:, :, 0:2 * GJ])
+            elif g > 1:
+                nc.sync.dma_start(out=out_v[a][:, :, GJ * g:GJ * (g + 1)], in_=o_t[a][:, :, GJ * g:GJ * (g + 1)])
 
         nc.vector.memset(warm[:], 0.0)
         nc.scalar.activation(out=warm[:], in_=warm[:], func=ACT.Exp)

@@ -20,12 +20,19 @@ NT = N // P
 PACK = 4
 GJ = 8
 XJ = 4
-FIRST = [1, 1, 2, 4]
-LAST = [4, 2, 1, 1]
+XC = J // XJ
+X_LOADS = 8
+BANK_J = 2
+
+FIRST_UNITS = [1, 1, 2, 4]
+BEFORE_LAST_UNITS = [4, 4]
+LAST_UNITS = [4, 2, 1, 1]
+
 PREFETCH = 4
-MX_START = 6
 X_STEP = 4
-N_EARLY = X_STEP + J // (2 * XJ) - 1
+MX_STEP = 6
+FIRST_MULTIPLY_UNITS = 5
+N_REGROUP = X_STEP + XC // 2 - 1
 N_LATE = 3
 
 
@@ -33,13 +40,13 @@ def make_units():
     units = []
     for a in range(NT):
         for g in range(J // GJ):
-            sizes = [8]
+            sizes = [GJ]
             if a == 0 and g == 0:
-                sizes = FIRST
+                sizes = FIRST_UNITS
             if a == NT - 1 and g == J // GJ - 2:
-                sizes = [4, 4]
+                sizes = BEFORE_LAST_UNITS
             if a == NT - 1 and g == J // GJ - 1:
-                sizes = LAST
+                sizes = LAST_UNITS
             j0 = g * GJ
             for nj in sizes:
                 units.append((a, j0, nj))
@@ -51,20 +58,26 @@ UNITS = make_units()
 NU = len(UNITS)
 
 
-def g_adds(u):
+def gpsimd_adds(u):
     nj = UNITS[u][2]
-    if 2 <= u < len(FIRST) + 1:
+    if nj == 1:
+        return 0
+    if u < FIRST_MULTIPLY_UNITS:
         return -(-nj // 3)
-    return nj // 4 if nj > 2 else nj // 2
+    return max(nj // 4, 1)
 
 
-def norm_engine(u, jj):
+def multiply_engine(u, jj):
     nj = UNITS[u][2]
     if u >= NU - N_LATE:
-        return "VS"[jj % 2]
-    if u < N_EARLY:
-        return "S" if 2 * jj < nj else "G"
-    return "S" if 4 * jj < nj else "G"
+        return "vector" if jj % 2 == 0 else "scalar"
+    scalar_share = 2 if u < N_REGROUP else 4
+    return "scalar" if scalar_share * jj < nj else "gpsimd"
+
+
+def copied_by_vector(u, i):
+    a, j0, nj = UNITS[u]
+    return a == NT - 1 and j0 // GJ == J // GJ - 2 and i % 2 == 1
 
 
 def tile_learnablemasktemporalaggregation_kernel(tc, x, learnable_offset, predefined_weights, out):
@@ -76,258 +89,264 @@ def tile_learnablemasktemporalaggregation_kernel(tc, x, learnable_offset, predef
 
     with ExitStack() as ctx:
         const = ctx.enter_context(tc.tile_pool(name="const", bufs=1))
-        ld = ctx.enter_context(tc.tile_pool(name="ld", bufs=PREFETCH + 1))
-        zp = ctx.enter_context(tc.tile_pool(name="zp", bufs=4))
-        st = ctx.enter_context(tc.tile_pool(name="st", bufs=6))
-        mp = ctx.enter_context(tc.tile_pool(name="mp", bufs=3))
-        gp = ctx.enter_context(tc.tile_pool(name="gp", bufs=2))
-        cp = ctx.enter_context(tc.tile_pool(name="cp", bufs=4))
-        op = ctx.enter_context(tc.tile_pool(name="op", bufs=2))
-        psum_c = ctx.enter_context(tc.psum_pool(name="psum_c", bufs=2))
-        psum_t = ctx.enter_context(tc.psum_pool(name="psum_t", bufs=4))
-        psum_o = ctx.enter_context(tc.psum_pool(name="psum_o", bufs=2))
+        off_pool = ctx.enter_context(tc.tile_pool(name="off_pool", bufs=PREFETCH + 1))
+        z_pool = ctx.enter_context(tc.tile_pool(name="z_pool", bufs=4))
+        stat_pool = ctx.enter_context(tc.tile_pool(name="stat_pool", bufs=6))
+        mask_pool = ctx.enter_context(tc.tile_pool(name="mask_pool", bufs=3))
+        grouped_pool = ctx.enter_context(tc.tile_pool(name="grouped_pool", bufs=2))
+        code_pool = ctx.enter_context(tc.tile_pool(name="code_pool", bufs=4))
+        out_pool = ctx.enter_context(tc.tile_pool(name="out_pool", bufs=2))
+        psum_pre = ctx.enter_context(tc.psum_pool(name="psum_pre", bufs=2))
+        psum_words = ctx.enter_context(tc.psum_pool(name="psum_words", bufs=4))
+        psum_out = ctx.enter_context(tc.psum_pool(name="psum_out", bufs=2))
         ctx.enter_context(tc.manual_schedule())
 
-        pre_t, off_t, z_t, nmax_t, ssum_t, rinv_t, mask_t = {}, {}, {}, {}, {}, {}, {}
-        pt_t, grp_t, codes_t, scl_t, po_t, o_t = {}, {}, {}, {}, {}, {}
+        off_t, z_t, neg_max, row_sum, inv_sum, mask_t = {}, {}, {}, {}, {}, {}
+        words_t, grouped_t, codes_t, scales_t = {}, {}, {}, {}
+        pre_t, o_t, product_t = {}, {}, {}
 
         x_raw = const.tile([P, B * PACK, J], BF16)
-        x_grp = const.tile([P, J, B * PACK], BF16, align_bytes=64)
+        x_grouped = const.tile([P, J, B * PACK], BF16, align_bytes=64)
         x_codes = const.tile([P, J * B], U32, align_bytes=64)
-        x_scl = const.tile([P, J * B], U8, align_bytes=64)
+        x_scales = const.tile([P, J * B], U8, align_bytes=64)
         pre_sb = const.tile([P, NT, N], BF16)
-        ident_f = const.tile([P, P], F32)
-        ident_b = const.tile([P, P], BF16)
+        ident_f32 = const.tile([P, P], F32)
+        ident_bf16 = const.tile([P, P], BF16)
         warm = const.tile([P, 1], F32)
-
-        def x_load(c):
-            nc.sync.dma_start(
-                out=x_raw[:, 32 * c:32 * (c + 1), :].rearrange("p (b t) j -> p b t j", t=PACK),
-                in_=x_v[:, 8 * c:8 * (c + 1), :, :],
-            )
-
-        def x_group(c):
-            nc.gpsimd.tensor_scalar(
-                out=x_grp[:, XJ * c:XJ * (c + 1), :].rearrange("p j (b t) -> p b j t", t=PACK),
-                in0=x_raw[:, :, XJ * c:XJ * (c + 1)].rearrange("p (b t) j -> p b j t", t=PACK),
-                scalar1=1.0, scalar2=0.0, op0=ALU.mult, op1=ALU.add,
-            )
-
-        def x_quant(c):
-            w = 2 * XJ * B
-            nc.vector.quantize_mx(
-                out=x_codes[:, w * c:w * (c + 1)].bitcast(FP8X4),
-                scales=x_scl[:, w * c:w * (c + 1)],
-                in_=x_grp[:, 2 * XJ * c:2 * XJ * (c + 1), :].rearrange("p j c -> p (j c)"),
-            )
 
         def load_pre(a):
             nc.sync.dma_start(out=pre_sb[:, a, :], in_=pre_v[a])
 
-        def pre_to_psum(a):
-            pre_t[a] = psum_c.tile([P, 1, N], BF16, name="pre_ps")
-            nc.tensor.matmul(out=pre_t[a][:, 0, :], lhsT=ident_b[:], rhs=pre_sb[:, a, :], start=True, stop=True)
-
-        def load(u):
+        def load_offset(u):
             a, j0, nj = UNITS[u]
-            off_t[u] = ld.tile([P, nj, N], BF16, name="off")
+            off_t[u] = off_pool.tile([P, nj, N], BF16, name="off")
             nc.sync.dma_start(out=off_t[u][:], in_=off_v[a][:, j0:j0 + nj, :])
 
-        def new_z(u):
-            z_t[u] = zp.tile([P, UNITS[u][2], N], F32, name="z")
-
-        def half(u):
-            return UNITS[u][2] // 2
-
-        def add(u, lo, hi):
-            if u not in z_t:
-                new_z(u)
-            if lo >= hi:
-                return
-            a = UNITS[u][0]
-            pre = pre_sb[:, a:a + 1, :] if u == 0 else pre_t[a][:]
-            nc.vector.tensor_tensor(
-                out=z_t[u][:, lo:hi, :], in0=off_t[u][:, lo:hi, :],
-                in1=pre.to_broadcast([P, hi - lo, N]), op=ALU.add,
+        def load_x(c):
+            n = B // X_LOADS
+            nc.sync.dma_start(
+                out=x_raw[:, n * PACK * c:n * PACK * (c + 1), :].rearrange("p (b t) j -> p b t j", t=PACK),
+                in_=x_v[:, n * c:n * (c + 1), :, :],
             )
 
-        def add_gpsimd(u):
+        def pre_to_psum(a):
+            pre_t[a] = psum_pre.tile([P, 1, N], BF16, name="pre_ps")
+            nc.tensor.matmul(out=pre_t[a][:, 0, :], lhsT=ident_bf16[:], rhs=pre_sb[:, a, :], start=True, stop=True)
+
+        def group_x(c):
+            joints = slice(XJ * c, XJ * (c + 1))
+            nc.gpsimd.tensor_scalar(
+                out=x_grouped[:, joints, :].rearrange("p j (b t) -> p b j t", t=PACK),
+                in0=x_raw[:, :, joints].rearrange("p (b t) j -> p b j t", t=PACK),
+                scalar1=1.0, scalar2=0.0, op0=ALU.mult, op1=ALU.add,
+            )
+
+        def quantize_x(c):
+            joints = slice(2 * XJ * c, 2 * XJ * (c + 1))
+            cols = slice(2 * XJ * B * c, 2 * XJ * B * (c + 1))
+            nc.vector.quantize_mx(
+                out=x_codes[:, cols].bitcast(FP8X4),
+                scales=x_scales[:, cols],
+                in_=x_grouped[:, joints, :].rearrange("p j c -> p (j c)"),
+            )
+
+        def add_on_gpsimd(u):
             a, j0, nj = UNITS[u]
-            new_z(u)
-            n = g_adds(u)
+            z_t[u] = z_pool.tile([P, nj, N], F32, name="z")
+            n = gpsimd_adds(u)
             if n > 0:
                 nc.gpsimd.tensor_tensor(
                     out=z_t[u][:, nj - n:nj, :], in0=off_t[u][:, nj - n:nj, :],
                     in1=pre_sb[:, a:a + 1, :].to_broadcast([P, n, N]), op=ALU.add,
                 )
 
-        def row_max(u, lo, hi):
-            if u not in nmax_t:
-                nmax_t[u] = st.tile([P, UNITS[u][2]], F32, name="nmax")
-            if lo >= hi:
-                return
-            nc.vector.tensor_reduce(
-                out=nmax_t[u][:, lo:hi], in_=z_t[u][:, lo:hi, :], axis=AX.X, op=ALU.max, negate=True,
+        def add_on_vector(u):
+            a, j0, nj = UNITS[u]
+            n = nj - gpsimd_adds(u)
+            pre = pre_sb[:, a:a + 1, :] if u == 0 else pre_t[a][:]
+            nc.vector.tensor_tensor(
+                out=z_t[u][:, 0:n, :], in0=off_t[u][:, 0:n, :], in1=pre.to_broadcast([P, n, N]), op=ALU.add,
             )
 
-        def exps(u, lo, hi):
-            if u not in ssum_t:
-                ssum_t[u] = st.tile([P, UNITS[u][2]], F32, name="ssum")
+        def halves(u):
+            nj = UNITS[u][2]
+            return (0, nj // 2), (nj // 2, nj)
+
+        def row_maxima(u):
+            neg_max[u] = stat_pool.tile([P, UNITS[u][2]], F32, name="neg_max")
+            for lo, hi in halves(u):
+                if lo < hi:
+                    nc.vector.tensor_reduce(
+                        out=neg_max[u][:, lo:hi], in_=z_t[u][:, lo:hi, :], axis=AX.X, op=ALU.max, negate=True,
+                    )
+
+        def exponentials(u, half):
+            if half == 0:
+                row_sum[u] = stat_pool.tile([P, UNITS[u][2]], F32, name="row_sum")
+            lo, hi = halves(u)[half]
             for jj in range(lo, hi):
                 nc.scalar.activation(
                     out=z_t[u][:, jj, :], in_=z_t[u][:, jj, :], func=ACT.Exp,
-                    bias=nmax_t[u][:, jj:jj + 1], scale=1.0, accum_out=ssum_t[u][:, jj:jj + 1],
+                    bias=neg_max[u][:, jj:jj + 1], scale=1.0, accum_out=row_sum[u][:, jj:jj + 1],
                 )
 
-        def recip(u):
+        def reciprocal(u):
             nj = UNITS[u][2]
-            rinv_t[u] = st.tile([P, nj], F32, name="rinv")
-            nc.vector.reciprocal(out=rinv_t[u][:], in_=ssum_t[u][:])
+            inv_sum[u] = stat_pool.tile([P, nj], F32, name="inv_sum")
+            nc.vector.reciprocal(out=inv_sum[u][:], in_=row_sum[u][:])
+            mask_t[u] = mask_pool.tile([P, nj, N], BF16, name="mask")
 
-        def norm(u, engine):
-            nj = UNITS[u][2]
-            if u not in mask_t:
-                mask_t[u] = mp.tile([P, nj, N], BF16, name="mask")
-            for jj in range(nj):
-                if norm_engine(u, jj) != engine:
+        def multiply(u, engine):
+            for jj in range(UNITS[u][2]):
+                if multiply_engine(u, jj) != engine:
                     continue
-                dst, src, r = mask_t[u][:, jj, :], z_t[u][:, jj, :], rinv_t[u][:, jj:jj + 1]
-                if engine == "V":
-                    nc.vector.tensor_scalar(out=dst, in0=src, scalar1=r, scalar2=None, op0=ALU.mult)
-                elif engine == "S":
-                    nc.scalar.activation(out=dst, in_=src, func=ACT.Copy, scale=r)
+                dst, src, factor = mask_t[u][:, jj, :], z_t[u][:, jj, :], inv_sum[u][:, jj:jj + 1]
+                if engine == "vector":
+                    nc.vector.tensor_scalar(out=dst, in0=src, scalar1=factor, scalar2=None, op0=ALU.mult)
+                elif engine == "scalar":
+                    nc.scalar.activation(out=dst, in_=src, func=ACT.Copy, scale=factor)
                 else:
-                    nc.gpsimd.tensor_scalar(out=dst, in0=src, scalar1=r, scalar2=0.0, op0=ALU.mult, op1=ALU.add)
+                    nc.gpsimd.tensor_scalar(
+                        out=dst, in0=src, scalar1=factor, scalar2=0.0, op0=ALU.mult, op1=ALU.add,
+                    )
 
-        def transp(u):
+        def transpose(u):
             nj = UNITS[u][2]
-            pt_t[u] = []
+            words_t[u] = []
             words = mask_t[u][:].rearrange("p j m -> p (j m)").bitcast(F32)
-            for j0 in range(0, nj, 2):
-                pt = psum_t.tile([P, 2, 2, P], F32, name="pt")
-                pt_t[u].append(pt)
-                for jj in range(j0, min(j0 + 2, nj)):
+            for j0 in range(0, nj, BANK_J):
+                bank = psum_words.tile([P, BANK_J, 2, P], F32, name="bank")
+                words_t[u].append(bank)
+                for jj in range(j0, min(j0 + BANK_J, nj)):
                     for e in range(2):
                         w0 = jj * (N // 2) + e
-                        nc.tensor.transpose(pt[:, jj - j0, e, :], words[:, w0:w0 + N // 2 - 1:2], ident_f[:])
+                        nc.tensor.transpose(bank[:, jj - j0, e, :], words[:, w0:w0 + N // 2 - 1:2], ident_f32[:])
 
-        def copy_out(u):
+        def copy_words(u, on_vector):
             nj = UNITS[u][2]
-            grp_t[u] = gp.tile([P, nj, P, PACK], BF16, name="grp", align_bytes=64)
-            words = grp_t[u][:].rearrange("p j n t -> p (j n t)").bitcast(F32)
-            for i, pt in enumerate(pt_t[u]):
-                q = min(2, nj - 2 * i)
-                dst = words[:, 2 * i * 2 * P:(2 * i + q) * 2 * P].rearrange("p (q n e) -> p q n e", q=q, e=2)
-                src = pt[:, 0:q, :, :].rearrange("p q e n -> p q n e")
-                nc.scalar.copy(out=dst, in_=src)
+            if u not in grouped_t:
+                grouped_t[u] = grouped_pool.tile([P, nj, P, PACK], BF16, name="grouped", align_bytes=64)
+            words = grouped_t[u][:].rearrange("p j n t -> p (j n t)").bitcast(F32)
+            for i, bank in enumerate(words_t[u]):
+                if copied_by_vector(u, i) != on_vector:
+                    continue
+                j0 = BANK_J * i
+                n = min(BANK_J, nj - j0)
+                dst = words[:, j0 * 2 * P:(j0 + n) * 2 * P].rearrange("p (q n e) -> p q n e", q=n, e=2)
+                src = bank[:, 0:n, :, :].rearrange("p q e n -> p q n e")
+                if on_vector:
+                    nc.vector.tensor_copy(out=dst, in_=src)
+                else:
+                    nc.scalar.copy(out=dst, in_=src)
 
-        def quant(u):
+        def quantize(u):
             nj = UNITS[u][2]
-            codes_t[u] = cp.tile([P, nj * P], U32, name="codes", align_bytes=64)
-            scl_t[u] = cp.tile([P, nj * P], U8, name="scl", align_bytes=64)
+            codes_t[u] = code_pool.tile([P, nj * P], U32, name="codes", align_bytes=64)
+            scales_t[u] = code_pool.tile([P, nj * P], U8, name="scales", align_bytes=64)
             nc.vector.quantize_mx(
-                out=codes_t[u][:].bitcast(FP8X4), scales=scl_t[u][:],
-                in_=grp_t[u][:].rearrange("p j n t -> p (j n t)"),
+                out=codes_t[u][:].bitcast(FP8X4), scales=scales_t[u][:],
+                in_=grouped_t[u][:].rearrange("p j n t -> p (j n t)"),
             )
 
-        def mx(u):
+        def multiply_mx(u):
             a, j0, nj = UNITS[u]
             g = (a, j0 // GJ)
             if j0 % GJ == 0:
-                po_t[g] = psum_o.tile([P, GJ, B], F32, name="po")
+                product_t[g] = psum_out.tile([P, GJ, B], F32, name="product")
             for jj in range(nj):
                 j = j0 + jj
                 nc.tensor.matmul_mx(
-                    out=po_t[g][:, j % GJ, :],
+                    out=product_t[g][:, j % GJ, :],
                     lhsT=codes_t[u][:, jj * P:(jj + 1) * P].bitcast(FP8X4),
-                    lhsT_scale=scl_t[u][:, jj * P:(jj + 1) * P],
+                    lhsT_scale=scales_t[u][:, jj * P:(jj + 1) * P],
                     rhs=x_codes[:, j * B:(j + 1) * B].bitcast(FP8X4),
-                    rhs_scale=x_scl[:, j * B:(j + 1) * B],
+                    rhs_scale=x_scales[:, j * B:(j + 1) * B],
                     start=True, stop=True,
                 )
 
-        def evac(u):
+        def store(u):
             a, j0, nj = UNITS[u]
             if (j0 + nj) % GJ != 0:
                 return
             g = j0 // GJ
             if g == 0:
-                o_t[a] = op.tile([P, B, J], F32, name="o_sb")
+                o_t[a] = out_pool.tile([P, B, J], F32, name="o")
+            joints = slice(GJ * g, GJ * (g + 1))
             last = a == NT - 1 and g == J // GJ - 1
             parts = [(0, B // 2, nc.sync), (B // 2, B, nc.scalar)] if last else [(0, B, nc.sync)]
             for lo, hi, queue in parts:
                 nc.scalar.copy(
-                    out=o_t[a][:, lo:hi, GJ * g:GJ * (g + 1)],
-                    in_=po_t[(a, g)][:, :, lo:hi].rearrange("p j b -> p b j"),
+                    out=o_t[a][:, lo:hi, joints],
+                    in_=product_t[(a, g)][:, :, lo:hi].rearrange("p j b -> p b j"),
                 )
                 if last:
-                    queue.dma_start(out=out_v[a][:, lo:hi, GJ * g:], in_=o_t[a][:, lo:hi, GJ * g:])
-            if last:
-                return
+                    queue.dma_start(out=out_v[a][:, lo:hi, joints], in_=o_t[a][:, lo:hi, joints])
             if a < NT - 1:
                 if g == J // GJ - 1:
                     nc.sync.dma_start(out=out_v[a], in_=o_t[a][:])
             elif g == 1:
                 nc.sync.dma_start(out=out_v[a][:, :, 0:2 * GJ], in_=o_t[a][:, :, 0:2 * GJ])
-            elif g > 1:
-                nc.sync.dma_start(out=out_v[a][:, :, GJ * g:GJ * (g + 1)], in_=o_t[a][:, :, GJ * g:GJ * (g + 1)])
+            elif g > 1 and not last:
+                nc.sync.dma_start(out=out_v[a][:, :, joints], in_=o_t[a][:, :, joints])
 
         nc.vector.memset(warm[:], 0.0)
         nc.scalar.activation(out=warm[:], in_=warm[:], func=ACT.Exp)
-        make_identity(nc, ident_f[:])
-        nc.vector.tensor_copy(out=ident_b[:], in_=ident_f[:])
+        make_identity(nc, ident_f32[:])
+        nc.vector.tensor_copy(out=ident_bf16[:], in_=ident_f32[:])
+
         load_pre(0)
-        for u in range(4):
-            load(u)
+        for u in range(len(FIRST_UNITS)):
+            load_offset(u)
         pre_to_psum(0)
-        for c in range(2):
-            x_load(c)
-        load(4)
+        load_x(0)
+        load_x(1)
+        load_offset(len(FIRST_UNITS))
         for c in range(2, 6):
-            x_load(c)
-        load(5)
-        for c in range(6, 8):
-            x_load(c)
+            load_x(c)
+        load_offset(len(FIRST_UNITS) + 1)
+        for c in range(6, X_LOADS):
+            load_x(c)
         for a in range(1, NT):
             load_pre(a)
 
         for k in range(-1, NU + 5):
-            if 6 <= k + PREFETCH < NU:
-                load(k + PREFETCH)
+            if len(FIRST_UNITS) + 2 <= k + PREFETCH < NU:
+                load_offset(k + PREFETCH)
             if 0 <= k - 1 < NU:
-                exps(k - 1, half(k - 1), UNITS[k - 1][2])
+                exponentials(k - 1, 1)
             if 0 <= k < NU:
-                add(k, 0, UNITS[k][2] - g_adds(k))
+                add_on_vector(k)
             if 0 <= k - 3 < NU:
-                quant(k - 3)
+                quantize(k - 3)
             if 0 <= k - 1 < NU:
-                recip(k - 1)
-                norm(k - 1, "V")
-                norm(k - 1, "G")
+                reciprocal(k - 1)
+                multiply(k - 1, "vector")
+                multiply(k - 1, "gpsimd")
             if 0 <= k - 2 < NU:
-                copy_out(k - 2)
-            if 0 <= k - 1 < NU:
-                norm(k - 1, "S")
+                copy_words(k - 2, on_vector=False)
             if k + 1 < NU:
-                add_gpsimd(k + 1)
-            if 0 <= k - X_STEP < J // (2 * XJ):
-                x_group(2 * (k - X_STEP))
-                x_group(2 * (k - X_STEP) + 1)
-            if 0 <= k - X_STEP - 1 < J // (2 * XJ):
-                x_quant(k - X_STEP - 1)
+                add_on_gpsimd(k + 1)
+            if 0 <= k - X_STEP < XC // 2:
+                group_x(2 * (k - X_STEP))
+                group_x(2 * (k - X_STEP) + 1)
+            if 0 <= k - X_STEP - 1 < XC // 2:
+                quantize_x(k - X_STEP - 1)
             if 0 <= k < NU:
-                row_max(k, 0, half(k))
-                row_max(k, half(k), UNITS[k][2])
+                row_maxima(k)
+            if 0 <= k - 2 < NU:
+                copy_words(k - 2, on_vector=True)
             if 0 <= k < NU - 2 and UNITS[k + 2][0] != UNITS[k + 1][0]:
                 pre_to_psum(UNITS[k + 2][0])
-            if k == MX_START:
-                for u in range(MX_START - 4):
-                    mx(u)
-            if k >= MX_START and k - 4 < NU:
-                mx(k - 4)
+            if k == MX_STEP:
+                for u in range(MX_STEP - 4):
+                    multiply_mx(u)
+            if MX_STEP <= k < NU + 4:
+                multiply_mx(k - 4)
             if 0 <= k - 4 < NU:
-                evac(k - 4)
-            if 0 <= k < NU:
-                exps(k, 0, half(k))
+                store(k - 4)
             if 0 <= k - 1 < NU:
-                transp(k - 1)
+                multiply(k - 1, "scalar")
+            if 0 <= k < NU:
+                exponentials(k, 0)
+            if 0 <= k - 1 < NU:
+                transpose(k - 1)

from contextlib import ExitStack

import concourse.mybir as mybir
from concourse.masks import make_identity

FLOPS = 2 * 64 * 512 * 512 * 32

BF16 = mybir.dt.bfloat16
F32 = mybir.dt.float32
U32 = mybir.dt.uint32
U8 = mybir.dt.uint8
FP8X4 = mybir.dt.float8_e4m3fn_x4
ALU = mybir.AluOpType
ACT = mybir.ActivationFunctionType
AX = mybir.AxisListType

P = 128
B, N, J = 64, 512, 32
NT = N // P
PACK = 4
GJ = 8
XJ = 4
XC = J // XJ
X_LOADS = 8
BANK_J = 2

FIRST_UNITS = [1, 1, 2, 4]
BEFORE_LAST_UNITS = [4, 4]
LAST_UNITS = [4, 2, 1, 1]

PREFETCH = 4
X_STEP = 4
MX_STEP = 6
FIRST_MULTIPLY_UNITS = 5
N_REGROUP = X_STEP + XC // 2 - 1
N_LATE = 3


def make_units():
    units = []
    for a in range(NT):
        for g in range(J // GJ):
            sizes = [GJ]
            if a == 0 and g == 0:
                sizes = FIRST_UNITS
            if a == NT - 1 and g == J // GJ - 2:
                sizes = BEFORE_LAST_UNITS
            if a == NT - 1 and g == J // GJ - 1:
                sizes = LAST_UNITS
            j0 = g * GJ
            for nj in sizes:
                units.append((a, j0, nj))
                j0 += nj
    return units


UNITS = make_units()
NU = len(UNITS)


def gpsimd_adds(u):
    nj = UNITS[u][2]
    if nj == 1:
        return 0
    if u < FIRST_MULTIPLY_UNITS:
        return -(-nj // 3)
    return max(nj // 4, 1)


def multiply_engine(u, jj):
    nj = UNITS[u][2]
    if u >= NU - N_LATE:
        return "vector" if jj % 2 == 0 else "scalar"
    scalar_share = 2 if u < N_REGROUP else 4
    return "scalar" if scalar_share * jj < nj else "gpsimd"


def copied_by_vector(u, i):
    a, j0, nj = UNITS[u]
    return a == NT - 1 and j0 // GJ == J // GJ - 2 and i % 2 == 1


def tile_learnablemasktemporalaggregation_kernel(tc, x, learnable_offset, predefined_weights, out):
    nc = tc.nc
    off_v = learnable_offset.rearrange("j (a p) m -> a p j m", p=P)
    pre_v = predefined_weights.rearrange("(a p) m -> a p m", p=P)
    x_v = x.rearrange("b (p t) j -> p b t j", t=PACK)
    out_v = out.rearrange("b (a p) j -> a p b j", p=P)

    with ExitStack() as ctx:
        const = ctx.enter_context(tc.tile_pool(name="const", bufs=1))
        off_pool = ctx.enter_context(tc.tile_pool(name="off_pool", bufs=PREFETCH + 1))
        z_pool = ctx.enter_context(tc.tile_pool(name="z_pool", bufs=4))
        stat_pool = ctx.enter_context(tc.tile_pool(name="stat_pool", bufs=6))
        mask_pool = ctx.enter_context(tc.tile_pool(name="mask_pool", bufs=3))
        grouped_pool = ctx.enter_context(tc.tile_pool(name="grouped_pool", bufs=2))
        code_pool = ctx.enter_context(tc.tile_pool(name="code_pool", bufs=4))
        out_pool = ctx.enter_context(tc.tile_pool(name="out_pool", bufs=2))
        psum_pre = ctx.enter_context(tc.psum_pool(name="psum_pre", bufs=2))
        psum_words = ctx.enter_context(tc.psum_pool(name="psum_words", bufs=4))
        psum_out = ctx.enter_context(tc.psum_pool(name="psum_out", bufs=2))
        ctx.enter_context(tc.manual_schedule())

        off_t, z_t, neg_max, row_sum, inv_sum, mask_t = {}, {}, {}, {}, {}, {}
        words_t, grouped_t, codes_t, scales_t = {}, {}, {}, {}
        pre_t, o_t, product_t = {}, {}, {}

        x_raw = const.tile([P, B * PACK, J], BF16)
        x_grouped = const.tile([P, J, B * PACK], BF16, align_bytes=64)
        x_codes = const.tile([P, J * B], U32, align_bytes=64)
        x_scales = const.tile([P, J * B], U8, align_bytes=64)
        pre_sb = const.tile([P, NT, N], BF16)
        ident_f32 = const.tile([P, P], F32)
        ident_bf16 = const.tile([P, P], BF16)
        warm = const.tile([P, 1], F32)

        def load_pre(a):
            nc.sync.dma_start(out=pre_sb[:, a, :], in_=pre_v[a])

        def load_offset(u):
            a, j0, nj = UNITS[u]
            off_t[u] = off_pool.tile([P, nj, N], BF16, name="off")
            nc.sync.dma_start(out=off_t[u][:], in_=off_v[a][:, j0:j0 + nj, :])

        def load_x(c):
            n = B // X_LOADS
            nc.sync.dma_start(
                out=x_raw[:, n * PACK * c:n * PACK * (c + 1), :].rearrange("p (b t) j -> p b t j", t=PACK),
                in_=x_v[:, n * c:n * (c + 1), :, :],
            )

        def pre_to_psum(a):
            pre_t[a] = psum_pre.tile([P, 1, N], BF16, name="pre_ps")
            nc.tensor.matmul(out=pre_t[a][:, 0, :], lhsT=ident_bf16[:], rhs=pre_sb[:, a, :], start=True, stop=True)

        def group_x(c):
            joints = slice(XJ * c, XJ * (c + 1))
            nc.gpsimd.tensor_scalar(
                out=x_grouped[:, joints, :].rearrange("p j (b t) -> p b j t", t=PACK),
                in0=x_raw[:, :, joints].rearrange("p (b t) j -> p b j t", t=PACK),
                scalar1=1.0, scalar2=0.0, op0=ALU.mult, op1=ALU.add,
            )

        def quantize_x(c):
            joints = slice(2 * XJ * c, 2 * XJ * (c + 1))
            cols = slice(2 * XJ * B * c, 2 * XJ * B * (c + 1))
            nc.vector.quantize_mx(
                out=x_codes[:, cols].bitcast(FP8X4),
                scales=x_scales[:, cols],
                in_=x_grouped[:, joints, :].rearrange("p j c -> p (j c)"),
            )

        def add_on_gpsimd(u):
            a, j0, nj = UNITS[u]
            z_t[u] = z_pool.tile([P, nj, N], F32, name="z")
            n = gpsimd_adds(u)
            if n > 0:
                nc.gpsimd.tensor_tensor(
                    out=z_t[u][:, nj - n:nj, :], in0=off_t[u][:, nj - n:nj, :],
                    in1=pre_sb[:, a:a + 1, :].to_broadcast([P, n, N]), op=ALU.add,
                )

        def add_on_vector(u):
            a, j0, nj = UNITS[u]
            n = nj - gpsimd_adds(u)
            pre = pre_sb[:, a:a + 1, :] if u == 0 else pre_t[a][:]
            nc.vector.tensor_tensor(
                out=z_t[u][:, 0:n, :], in0=off_t[u][:, 0:n, :], in1=pre.to_broadcast([P, n, N]), op=ALU.add,
            )

        def halves(u):
            nj = UNITS[u][2]
            return (0, nj // 2), (nj // 2, nj)

        def row_maxima(u):
            neg_max[u] = stat_pool.tile([P, UNITS[u][2]], F32, name="neg_max")
            for lo, hi in halves(u):
                if lo < hi:
                    nc.vector.tensor_reduce(
                        out=neg_max[u][:, lo:hi], in_=z_t[u][:, lo:hi, :], axis=AX.X, op=ALU.max, negate=True,
                    )

        def exponentials(u, half):
            if half == 0:
                row_sum[u] = stat_pool.tile([P, UNITS[u][2]], F32, name="row_sum")
            lo, hi = halves(u)[half]
            for jj in range(lo, hi):
                nc.scalar.activation(
                    out=z_t[u][:, jj, :], in_=z_t[u][:, jj, :], func=ACT.Exp,
                    bias=neg_max[u][:, jj:jj + 1], scale=1.0, accum_out=row_sum[u][:, jj:jj + 1],
                )

        def reciprocal(u):
            nj = UNITS[u][2]
            inv_sum[u] = stat_pool.tile([P, nj], F32, name="inv_sum")
            nc.vector.reciprocal(out=inv_sum[u][:], in_=row_sum[u][:])
            mask_t[u] = mask_pool.tile([P, nj, N], BF16, name="mask")

        def multiply(u, engine):
            for jj in range(UNITS[u][2]):
                if multiply_engine(u, jj) != engine:
                    continue
                dst, src, factor = mask_t[u][:, jj, :], z_t[u][:, jj, :], inv_sum[u][:, jj:jj + 1]
                if engine == "vector":
                    nc.vector.tensor_scalar(out=dst, in0=src, scalar1=factor, scalar2=None, op0=ALU.mult)
                elif engine == "scalar":
                    nc.scalar.activation(out=dst, in_=src, func=ACT.Copy, scale=factor)
                else:
                    nc.gpsimd.tensor_scalar(
                        out=dst, in0=src, scalar1=factor, scalar2=0.0, op0=ALU.mult, op1=ALU.add,
                    )

        def transpose(u):
            nj = UNITS[u][2]
            words_t[u] = []
            words = mask_t[u][:].rearrange("p j m -> p (j m)").bitcast(F32)
            for j0 in range(0, nj, BANK_J):
                bank = psum_words.tile([P, BANK_J, 2, P], F32, name="bank")
                words_t[u].append(bank)
                for jj in range(j0, min(j0 + BANK_J, nj)):
                    for e in range(2):
                        w0 = jj * (N // 2) + e
                        nc.tensor.transpose(bank[:, jj - j0, e, :], words[:, w0:w0 + N // 2 - 1:2], ident_f32[:])

        def copy_words(u, on_vector):
            nj = UNITS[u][2]
            if u not in grouped_t:
                grouped_t[u] = grouped_pool.tile([P, nj, P, PACK], BF16, name="grouped", align_bytes=64)
            words = grouped_t[u][:].rearrange("p j n t -> p (j n t)").bitcast(F32)
            for i, bank in enumerate(words_t[u]):
                if copied_by_vector(u, i) != on_vector:
                    continue
                j0 = BANK_J * i
                n = min(BANK_J, nj - j0)
                dst = words[:, j0 * 2 * P:(j0 + n) * 2 * P].rearrange("p (q n e) -> p q n e", q=n, e=2)
                src = bank[:, 0:n, :, :].rearrange("p q e n -> p q n e")
                if on_vector:
                    nc.vector.tensor_copy(out=dst, in_=src)
                else:
                    nc.scalar.copy(out=dst, in_=src)

        def quantize(u):
            nj = UNITS[u][2]
            codes_t[u] = code_pool.tile([P, nj * P], U32, name="codes", align_bytes=64)
            scales_t[u] = code_pool.tile([P, nj * P], U8, name="scales", align_bytes=64)
            nc.vector.quantize_mx(
                out=codes_t[u][:].bitcast(FP8X4), scales=scales_t[u][:],
                in_=grouped_t[u][:].rearrange("p j n t -> p (j n t)"),
            )

        def multiply_mx(u):
            a, j0, nj = UNITS[u]
            g = (a, j0 // GJ)
            if j0 % GJ == 0:
                product_t[g] = psum_out.tile([P, GJ, B], F32, name="product")
            for jj in range(nj):
                j = j0 + jj
                nc.tensor.matmul_mx(
                    out=product_t[g][:, j % GJ, :],
                    lhsT=codes_t[u][:, jj * P:(jj + 1) * P].bitcast(FP8X4),
                    lhsT_scale=scales_t[u][:, jj * P:(jj + 1) * P],
                    rhs=x_codes[:, j * B:(j + 1) * B].bitcast(FP8X4),
                    rhs_scale=x_scales[:, j * B:(j + 1) * B],
                    start=True, stop=True,
                )

        def store(u):
            a, j0, nj = UNITS[u]
            if (j0 + nj) % GJ != 0:
                return
            g = j0 // GJ
            if g == 0:
                o_t[a] = out_pool.tile([P, B, J], F32, name="o")
            joints = slice(GJ * g, GJ * (g + 1))
            last = a == NT - 1 and g == J // GJ - 1
            parts = [(0, B // 2, nc.sync), (B // 2, B, nc.scalar)] if last else [(0, B, nc.sync)]
            for lo, hi, queue in parts:
                nc.scalar.copy(
                    out=o_t[a][:, lo:hi, joints],
                    in_=product_t[(a, g)][:, :, lo:hi].rearrange("p j b -> p b j"),
                )
                if last:
                    queue.dma_start(out=out_v[a][:, lo:hi, joints], in_=o_t[a][:, lo:hi, joints])
            if a < NT - 1:
                if g == J // GJ - 1:
                    nc.sync.dma_start(out=out_v[a], in_=o_t[a][:])
            elif g == 1:
                nc.sync.dma_start(out=out_v[a][:, :, 0:2 * GJ], in_=o_t[a][:, :, 0:2 * GJ])
            elif g > 1 and not last:
                nc.sync.dma_start(out=out_v[a][:, :, joints], in_=o_t[a][:, :, joints])

        nc.vector.memset(warm[:], 0.0)
        nc.scalar.activation(out=warm[:], in_=warm[:], func=ACT.Exp)
        make_identity(nc, ident_f32[:])
        nc.vector.tensor_copy(out=ident_bf16[:], in_=ident_f32[:])

        load_pre(0)
        for u in range(len(FIRST_UNITS)):
            load_offset(u)
        pre_to_psum(0)
        load_x(0)
        load_x(1)
        load_offset(len(FIRST_UNITS))
        for c in range(2, 6):
            load_x(c)
        load_offset(len(FIRST_UNITS) + 1)
        for c in range(6, X_LOADS):
            load_x(c)
        for a in range(1, NT):
            load_pre(a)

        for k in range(-1, NU + 5):
            if len(FIRST_UNITS) + 2 <= k + PREFETCH < NU:
                load_offset(k + PREFETCH)
            if 0 <= k - 1 < NU:
                exponentials(k - 1, 1)
            if 0 <= k < NU:
                add_on_vector(k)
            if 0 <= k - 3 < NU:
                quantize(k - 3)
            if 0 <= k - 1 < NU:
                reciprocal(k - 1)
                multiply(k - 1, "vector")
                multiply(k - 1, "gpsimd")
            if 0 <= k - 2 < NU:
                copy_words(k - 2, on_vector=False)
            if k + 1 < NU:
                add_on_gpsimd(k + 1)
            if 0 <= k - X_STEP < XC // 2:
                group_x(2 * (k - X_STEP))
                group_x(2 * (k - X_STEP) + 1)
            if 0 <= k - X_STEP - 1 < XC // 2:
                quantize_x(k - X_STEP - 1)
            if 0 <= k < NU:
                row_maxima(k)
            if 0 <= k - 2 < NU:
                copy_words(k - 2, on_vector=True)
            if 0 <= k < NU - 2 and UNITS[k + 2][0] != UNITS[k + 1][0]:
                pre_to_psum(UNITS[k + 2][0])
            if k == MX_STEP:
                for u in range(MX_STEP - 4):
                    multiply_mx(u)
            if MX_STEP <= k < NU + 4:
                multiply_mx(k - 4)
            if 0 <= k - 4 < NU:
                store(k - 4)
            if 0 <= k - 1 < NU:
                multiply(k - 1, "scalar")
            if 0 <= k < NU:
                exponentials(k, 0)
            if 0 <= k - 1 < NU:
                transpose(k - 1)
